import numpy as np
import ml_dtypes


def mxq(x, axis, fmt="e4m3"):
    dtype, down = {"e4m3": (ml_dtypes.float8_e4m3fn, 7), "e5m2": (ml_dtypes.float8_e5m2, 14)}[fmt]
    v = np.moveaxis(np.asarray(x, np.float32).astype(ml_dtypes.bfloat16).astype(np.float64), axis, -1)
    blocks = v.reshape(v.shape[:-1] + (-1, 32))
    amax = np.abs(blocks).max(-1, keepdims=True)
    byte = np.maximum(np.where(amax > 0, np.frexp(amax)[1] - 1 + 127, 0) - down, 1)
    scale = np.exp2(byte - 127.0)
    codes = (blocks / scale).astype(np.float32).astype(dtype).astype(np.float64)
    return np.moveaxis((codes * scale).reshape(v.shape), -1, axis)


WIDE = False


def mx_kscale(k):
    if not WIDE:
        return np.ones(k)
    levels = np.array([10, -10, 5, -5, 0])
    if k % 512:
        return np.exp2(np.random.permutation(np.resize(levels, k // 32))).repeat(32)
    a = np.empty((k // 512, 16))
    for p in range(k // 512):
        a[p, :8] = np.random.permutation(np.resize(levels, 8))
        for g in range(8):
            far = levels[np.abs(levels - a[p, g]) >= 10]
            a[p, g + 8] = far[np.random.randint(len(far))]
    return np.exp2(a.ravel()).repeat(32)


BF16 = ml_dtypes.bfloat16


def bf(x):
    return np.asarray(x, np.float32).astype(BF16)


def f64(x):
    return np.asarray(x).astype(np.float64)


B, D0, D1, D2, D3, D4 = 8192, 512, 512, 512, 1024, 256
DENSITY = 0.02


def draw0():
    s, t = mx_kscale(D0), mx_kscale(D1)
    bound0 = np.sqrt(3.0 / (DENSITY * D0))
    bound1 = np.sqrt(6.0 / (DENSITY * D1))
    return {"x": bf(np.random.standard_normal((B, D0)) * s),
            "W0": bf(np.random.uniform(-bound0, bound0, (D1, D0)) / s[None, :] * t[:, None]),
            "b0": bf(np.random.standard_normal(D1) * 0.3 * t),
            "m0": bf(np.random.uniform(size=(D1, D0)) < DENSITY),
            "W1": bf(np.random.uniform(-bound1, bound1, (D2, D1)) / t[None, :]),
            "b1": bf(np.random.standard_normal(D2) * 0.3),
            "m1": bf(np.random.uniform(size=(D2, D1)) < DENSITY)}


def core(x, W0, b0, m0, W1, b1, m1):
    h = f64(x).reshape(x.shape[0], -1)
    w0 = f64(W0) * f64(m0)
    pre0 = (mxq(h, 1, "e4m3") @ mxq(w0, 1, "e4m3").T) + f64(b0)
    h0 = np.maximum(pre0, 0.0)
    w1 = f64(W1) * f64(m1)
    pre1 = (mxq(h0, 1, "e4m3") @ mxq(w1, 1, "e4m3").T) + f64(b1)
    return np.maximum(pre1, 0.0)


def e4m3fn_bytes(y):
    return np.clip(np.asarray(y, np.float64), -448.0, 448.0).astype(np.float32).astype(ml_dtypes.float8_e4m3fn).view(np.uint8)


def e4m3fn_values(b):
    return np.asarray(b, np.uint8).view(ml_dtypes.float8_e4m3fn).astype(np.float64)


def setup_inputs():
    d = draw0()
    x0 = np.asarray(d['x']).astype(np.float64)
    s = (np.max(np.abs(x0), axis=(0,), keepdims=True) / 448.0).astype(np.float32)
    out = {}
    for k, v in d.items():
        if k == 'x':
            out['x_bytes'] = e4m3fn_bytes(x0 / s.astype(np.float64))
            out['x_scale'] = s
        else:
            out[k] = v
    return out


def reference(x_bytes, x_scale, W0, b0, m0, W1, b1, m1):
    return core(e4m3fn_values(x_bytes) * x_scale.astype(np.float64), W0, b0, m0, W1, b1, m1)

@@ -1,0 +1,283 @@
+from contextlib import ExitStack
+
+import concourse.mybir as mybir
+from concourse.masks import make_identity
+
+F32 = mybir.dt.float32
+BF16 = mybir.dt.bfloat16
+U32 = mybir.dt.uint32
+U8 = mybir.dt.uint8
+F8 = mybir.dt.float8_e4m3fn
+FP8X4 = mybir.dt.float8_e4m3fn_x4
+ALU = mybir.AluOpType
+ACT = mybir.ActivationFunctionType
+
+P = 128
+B, D = 8192, 512
+GROUP = 512
+NG = B // GROUP
+FLOPS = 2 * B * D * D * 2
+
+
+def tile_patchedsparsenetwork_pa_t_kernel(tc, x_bytes, x_scale, W0, b0, m0, W1, b1, m1, out):
+    nc = tc.nc
+    with ExitStack() as ctx:
+        keep = ctx.enter_context(tc.tile_pool(name="keep", bufs=1))
+        work = ctx.enter_context(tc.tile_pool(name="work", bufs=3))
+        psum = ctx.enter_context(tc.psum_pool(name="psum", bufs=2))
+
+        scale = keep.tile([P, 2 * D], F32, name="scale", align_bytes=64)
+        nc.scalar.dma_start(out=scale[:, 0:D], in_=x_scale.rearrange("o k -> (o k)").partition_broadcast(P))
+        warm = keep.tile([P, 1], F32, name="warm", align_bytes=64)
+        nc.vector.memset(warm[:], 0.0)
+        nc.scalar.activation(out=warm[:], in_=warm[:], func=ACT.Relu)
+        b0h = keep.tile([P, 4], BF16, name="b0h", align_bytes=64)
+        nc.scalar.dma_start(out=b0h[:], in_=b0.rearrange("(p t) -> p t", t=4))
+        b1h = keep.tile([P, 4], BF16, name="b1h", align_bytes=64)
+        nc.scalar.dma_start(out=b1h[:], in_=b1.rearrange("(p t) -> p t", t=4))
+
+        raw = {}
+
+        def load_w(key, src):
+            t = keep.tile([P, 4 * D], BF16, name=key, align_bytes=64)
+            nc.sync.dma_start(out=t[:], in_=src.rearrange("(m t) k -> m (t k)", t=4))
+            raw[key] = t
+
+        x8 = {}
+
+        def load_x(g):
+            t = keep.tile([P, 4 * D], U8, name="x8_%d" % g, align_bytes=64)
+            rows = x_bytes[g * GROUP : (g + 1) * GROUP, :]
+            nc.sync.dma_start(out=t[:], in_=rows.rearrange("(r j) k -> r (j k)", j=4))
+            x8[g] = t
+
+        load_w("w0", W0)
+        load_w("m0", m0)
+        load_x(0)
+        load_x(1)
+        load_w("w1", W1)
+        load_w("m1", m1)
+        for g in range(2, NG):
+            load_x(g)
+
+        ident = keep.tile([P, P], F32, name="ident", align_bytes=64)
+        make_identity(nc, ident[:])
+
+        nc.scalar.copy(out=scale[:, D : 2 * D], in_=scale[:, 0:D])
+        b0f = keep.tile([P, 4], F32, name="b0f", align_bytes=64)
+        nc.scalar.copy(out=b0f[:], in_=b0h[:])
+        b1f = keep.tile([P, 4], F32, name="b1f", align_bytes=64)
+        nc.scalar.copy(out=b1f[:], in_=b1h[:])
+        b0t = keep.tile([P, P, 4], F32, name="b0t", align_bytes=64)
+        nc.scalar.copy(out=b0t[:], in_=b0f[:].unsqueeze(1).to_broadcast([P, P, 4]))
+
+        natural, inter, codes, scales = {}, {}, {}, {}
+        xt_bank = {}
+
+        def new_natural(key):
+            natural[key] = work.tile([P, 4 * D], BF16, name="nat", tag="nat", align_bytes=64)
+
+        def mask_w(key, w, m):
+            new_natural(key)
+            nc.vector.tensor_tensor(out=natural[key][:], in0=raw[w][:], in1=raw[m][:], op=ALU.mult)
+
+        def widen(g, h):
+            if h == 0:
+                new_natural(g)
+            c = slice(2 * h * D, 2 * (h + 1) * D)
+            nc.vector.tensor_tensor(out=natural[g][:, c], in0=x8[g][:, c].bitcast(F8), in1=scale[:], op=ALU.mult)
+
+        def turn(key, h):
+            bank = psum.tile([P, 2, 2, P], F32, name="xt", tag="xt")
+            words = natural[key][:].bitcast(F32)
+            for jj in range(2):
+                base = 256 * (2 * h + jj)
+                for u in range(2):
+                    nc.tensor.transpose(bank[:, jj, u, :], words[:, base + u : base + 256 : 2], ident[:])
+            xt_bank[key, h] = bank
+
+        def turn_out(key, h):
+            if h == 0:
+                inter[key] = work.tile([P, 4 * D], BF16, name="inter", tag="inter", align_bytes=64)
+            dst = inter[key][:, 1024 * h : 1024 * (h + 1)].bitcast(F32)
+            nc.scalar.copy(
+                out=dst.rearrange("p (j r u) -> p j r u", j=2, u=2),
+                in_=xt_bank[key, h][:].rearrange("p j u r -> p j r u"),
+            )
+
+        def quantize(key, src, pool, tag):
+            codes[key] = pool.tile([P, D], U32, name="c_" + tag, tag="c_" + tag, align_bytes=64)
+            scales[key] = pool.tile([P, D], U8, name="s_" + tag, tag="s_" + tag, align_bytes=64)
+            nc.vector.quantize_mx(out=codes[key][:].bitcast(FP8X4), scales=scales[key][:], in_=src[:])
+
+        def mm(dst, lkey, lcols, rkey, rcols):
+            nc.tensor.matmul_mx(
+                out=dst,
+                lhsT=codes[lkey][:, lcols].bitcast(FP8X4),
+                lhsT_scale=scales[lkey][:, lcols],
+                rhs=codes[rkey][:, rcols].bitcast(FP8X4),
+                rhs_scale=scales[rkey][:, rcols],
+                start=True,
+                stop=True,
+            )
+
+        h_bank, h_sb = {}, {}
+
+        def layer1(g, j):
+            bank = psum.tile([P, 4, P], F32, name="hb", tag="hb")
+            for t in range(4):
+                mm(bank[:, t, :], "W0", slice(P * t, P * (t + 1)), g, slice(P * j, P * (j + 1)))
+            h_bank[g, j] = bank
+
+        def bias1(g, j):
+            if j == 0:
+                h_sb[g] = work.tile([P, 4 * D], BF16, name="h_sb", tag="h_sb", align_bytes=64)
+            dst = h_sb[g][:, j * D : (j + 1) * D].rearrange("p (n t) -> p n t", t=4)
+            nc.vector.tensor_tensor(out=dst, in0=h_bank[g, j][:].rearrange("p t n -> p n t"), in1=b0t[:], op=ALU.add)
+
+        h_planes = {}
+
+        def bias_relu1(g, j):
+            h_planes[g] = work.tile([P, 4, P], BF16, name="h_pl", tag="h_pl", align_bytes=64)
+            for t in range(4):
+                nc.scalar.activation(
+                    out=h_planes[g][:, t, :], in_=h_bank[g, j][:, t, :], func=ACT.Relu, bias=b0f[:, t : t + 1]
+                )
+
+        def interleave1(g, j):
+            dst = h_sb[g][:, j * D : (j + 1) * D].rearrange("p (n t) -> p n t", t=4)
+            nc.vector.tensor_copy(out=dst, in_=h_planes[g][:].rearrange("p t n -> p n t"))
+
+        def relu1(g):
+            nc.vector.tensor_scalar_max(h_sb[g][:, 0 : 3 * D], h_sb[g][:, 0 : 3 * D], 0.0)
+
+        o_bank, y_sb, t_bank, o_sb = {}, {}, {}, {}
+
+        def layer2(g, t):
+            bank = psum.tile([P, GROUP], F32, name="ob", tag="ob")
+            mm(bank[:], "W1", slice(P * t, P * (t + 1)), ("h", g), slice(0, GROUP))
+            o_bank[g, t] = bank
+
+        def bias2(g, t, vec):
+            if t == 0:
+                y_sb[g] = work.tile([P, 4, GROUP], F32, name="y_sb", tag="y_sb", align_bytes=64)
+            if vec:
+                nc.vector.tensor_scalar(
+                    out=y_sb[g][:, t, :], in0=o_bank[g, t][:], scalar1=b1f[:, t : t + 1], scalar2=0.0, op0=ALU.add, op1=ALU.max
+                )
+            else:
+                nc.scalar.activation(out=y_sb[g][:, t, :], in_=o_bank[g, t][:], func=ACT.Relu, bias=b1f[:, t : t + 1])
+
+        def back(g, j):
+            bank = psum.tile([P, 4, P], F32, name="tb", tag="tb")
+            for t in range(4):
+                nc.tensor.transpose(bank[:, t, :], y_sb[g][:, t, P * j : P * (j + 1)], ident[:])
+            t_bank[g, j] = bank
+
+        def back_out(g, j, vec):
+            if j == 0:
+                o_sb[g] = work.tile([P, 4, D], F32, name="o_sb", tag="o_sb", align_bytes=64)
+            dst = o_sb[g][:, j, :].rearrange("p (c t) -> p c t", t=4)
+            src = t_bank[g, j][:].rearrange("p t c -> p c t")
+            if vec:
+                nc.vector.tensor_copy(out=dst, in_=src)
+            else:
+                nc.scalar.copy(out=dst, in_=src)
+
+        def store(g, j0, j1):
+            rows = out[g * GROUP : (g + 1) * GROUP, :].rearrange("(r j) c -> r j c", j=4)
+            nc.sync.dma_start(out=rows[:, j0:j1, :], in_=o_sb[g][:, j0:j1, :])
+
+        def ok(g):
+            return 0 <= g < NG
+
+        mask_w("W0", "w0", "m0")
+        for h in range(2):
+            turn("W0", h)
+            turn_out("W0", h)
+        widen(0, 0)
+        widen(0, 1)
+        for h in range(2):
+            turn(0, h)
+            turn_out(0, h)
+        quantize("W0", inter["W0"], keep, "w0")
+        widen(1, 0)
+        quantize(0, inter[0], work, "x")
+        layer1(0, 0)
+        layer1(0, 1)
+        widen(1, 1)
+        mask_w("W1", "w1", "m1")
+        for h in range(2):
+            turn("W1", h)
+            turn_out("W1", h)
+
+        for i in range(NG + 2):
+            cur, nxt, nx2, prv, pp = ok(i), ok(i + 1), ok(i + 2), ok(i - 1), ok(i - 2)
+            tail = i >= NG
+            if nxt:
+                turn(i + 1, 0)
+            if pp:
+                back(i - 2, 0)
+            if nxt:
+                turn_out(i + 1, 0)
+            if pp:
+                back_out(i - 2, 0, tail)
+            if cur:
+                bias1(i, 0)
+            if prv:
+                layer2(i - 1, 0)
+                layer2(i - 1, 1)
+            if cur:
+                layer1(i, 2)
+                bias1(i, 1)
+            if nx2:
+                widen(i + 2, 0)
+            if prv:
+                bias2(i - 1, 0, False)
+            if nxt:
+                turn(i + 1, 1)
+            if pp:
+                back(i - 2, 1)
+            if nxt:
+                turn_out(i + 1, 1)
+            if prv:
+                bias2(i - 1, 1, tail)
+            if pp:
+                back_out(i - 2, 1, False)
+            if cur:
+                layer1(i, 3)
+                bias_relu1(i, 3)
+            if prv:
+                layer2(i - 1, 2)
+                layer2(i - 1, 3)
+            if cur:
+                bias1(i, 2)
+            if prv:
+                bias2(i - 1, 2, False)
+                bias2(i - 1, 3, tail)
+            if pp:
+                back(i - 2, 2)
+                back(i - 2, 3)
+            if i == 0:
+                quantize("W1", inter["W1"], keep, "w1")
+            if nxt:
+                quantize(i + 1, inter[i + 1], work, "x")
+            if cur:
+                relu1(i)
+                interleave1(i, 3)
+            if nx2:
+                widen(i + 2, 1)
+            if cur:
+                quantize(("h", i), h_sb[i], work, "h")
+            if pp:
+                back_out(i - 2, 2, tail)
+                back_out(i - 2, 3, False)
+            if nxt:
+                layer1(i + 1, 0)
+                layer1(i + 1, 1)
+            if pp:
+                if tail:
+                    store(i - 2, 0, 2)
+                    store(i - 2, 2, 4)
+                else:
+                    store(i - 2, 0, 4)

@@ -14,6 +14,7 @@ ACT = mybir.ActivationFunctionType
 
 P = 128
 B, D = 8192, 512
+HALF = D // 2
 GROUP = 512
 NG = B // GROUP
 FLOPS = 2 * B * D * D * 2
@@ -24,7 +25,8 @@ def tile_patchedsparsenetwork_pa_t_kernel(tc, x_bytes, x_scale, W0, b0, m0, W1, 
     with ExitStack() as ctx:
         keep = ctx.enter_context(tc.tile_pool(name="keep", bufs=1))
         work = ctx.enter_context(tc.tile_pool(name="work", bufs=3))
-        psum = ctx.enter_context(tc.psum_pool(name="psum", bufs=2))
+        psum = ctx.enter_context(tc.psum_pool(name="psum", bufs=8))
+        ctx.enter_context(tc.manual_schedule())
 
         scale = keep.tile([P, 2 * D], F32, name="scale", align_bytes=64)
         nc.scalar.dma_start(out=scale[:, 0:D], in_=x_scale.rearrange("o k -> (o k)").partition_broadcast(P))
@@ -33,14 +35,20 @@ def tile_patchedsparsenetwork_pa_t_kernel(tc, x_bytes, x_scale, W0, b0, m0, W1, 
         nc.scalar.activation(out=warm[:], in_=warm[:], func=ACT.Relu)
         b0h = keep.tile([P, 4], BF16, name="b0h", align_bytes=64)
         nc.scalar.dma_start(out=b0h[:], in_=b0.rearrange("(p t) -> p t", t=4))
-        b1h = keep.tile([P, 4], BF16, name="b1h", align_bytes=64)
-        nc.scalar.dma_start(out=b1h[:], in_=b1.rearrange("(p t) -> p t", t=4))
+        b1h = keep.tile([P, 2], BF16, name="b1h", align_bytes=64)
+        nc.scalar.dma_start(out=b1h[:], in_=b1[0:HALF].rearrange("(m e) -> m e", e=2))
+        b1w = keep.tile([P, HALF], BF16, name="b1w", align_bytes=64)
+        nc.scalar.dma_start(out=b1w[:], in_=b1[HALF:D].partition_broadcast(P))
 
         raw = {}
 
-        def load_w(key, src):
-            t = keep.tile([P, 4 * D], BF16, name=key, align_bytes=64)
-            nc.sync.dma_start(out=t[:], in_=src.rearrange("(m t) k -> m (t k)", t=4))
+        def load_w(key, src, split):
+            t = keep.tile([P, 4, D], BF16, name=key, align_bytes=64)
+            if split:
+                nc.sync.dma_start(out=t[:, 0:2, :], in_=src[0:HALF, :].rearrange("(m e) k -> m e k", e=2))
+                nc.sync.dma_start(out=t[:, 2:4, :], in_=src[HALF:D, :].rearrange("(e m) k -> m e k", e=2))
+            else:
+                nc.sync.dma_start(out=t[:], in_=src.rearrange("(m t) k -> m t k", t=4))
             raw[key] = t
 
         x8 = {}
@@ -51,35 +59,40 @@ def tile_patchedsparsenetwork_pa_t_kernel(tc, x_bytes, x_scale, W0, b0, m0, W1, 
             nc.sync.dma_start(out=t[:], in_=rows.rearrange("(r j) k -> r (j k)", j=4))
             x8[g] = t
 
-        load_w("w0", W0)
-        load_w("m0", m0)
         load_x(0)
+        load_w("w0", W0, False)
+        load_w("m0", m0, False)
         load_x(1)
-        load_w("w1", W1)
-        load_w("m1", m1)
+        load_w("w1", W1, True)
+        load_w("m1", m1, True)
         for g in range(2, NG):
             load_x(g)
 
         ident = keep.tile([P, P], F32, name="ident", align_bytes=64)
         make_identity(nc, ident[:])
-
         nc.scalar.copy(out=scale[:, D : 2 * D], in_=scale[:, 0:D])
         b0f = keep.tile([P, 4], F32, name="b0f", align_bytes=64)
         nc.scalar.copy(out=b0f[:], in_=b0h[:])
-        b1f = keep.tile([P, 4], F32, name="b1f", align_bytes=64)
+        b1f = keep.tile([P, 2], F32, name="b1f", align_bytes=64)
         nc.scalar.copy(out=b1f[:], in_=b1h[:])
-        b0t = keep.tile([P, P, 4], F32, name="b0t", align_bytes=64)
-        nc.scalar.copy(out=b0t[:], in_=b0f[:].unsqueeze(1).to_broadcast([P, P, 4]))
+        b1t = keep.tile([P, 2, HALF], F32, name="b1t", align_bytes=64)
+        nc.scalar.copy(out=b1t[:], in_=b1w[:].unsqueeze(1).to_broadcast([P, 2, HALF]))
 
         natural, inter, codes, scales = {}, {}, {}, {}
-        xt_bank = {}
+        banks = {}
+
+        def bank(key, shape):
+            banks[key] = psum.tile(shape, F32, name="bank", tag="bank")
+            return banks[key]
 
         def new_natural(key):
             natural[key] = work.tile([P, 4 * D], BF16, name="nat", tag="nat", align_bytes=64)
 
         def mask_w(key, w, m):
             new_natural(key)
-            nc.vector.tensor_tensor(out=natural[key][:], in0=raw[w][:], in1=raw[m][:], op=ALU.mult)
+            nc.vector.tensor_tensor(
+                out=natural[key][:].rearrange("p (t k) -> p t k", t=4), in0=raw[w][:], in1=raw[m][:], op=ALU.mult
+            )
 
         def widen(g, h):
             if h == 0:
@@ -87,23 +100,29 @@ def tile_patchedsparsenetwork_pa_t_kernel(tc, x_bytes, x_scale, W0, b0, m0, W1, 
             c = slice(2 * h * D, 2 * (h + 1) * D)
             nc.vector.tensor_tensor(out=natural[g][:, c], in0=x8[g][:, c].bitcast(F8), in1=scale[:], op=ALU.mult)
 
+        def widen_block(g, j):
+            if j == 0:
+                new_natural(g)
+            c = slice(j * D, (j + 1) * D)
+            nc.vector.tensor_tensor(out=natural[g][:, c], in0=x8[g][:, c].bitcast(F8), in1=scale[:, 0:D], op=ALU.mult)
+
         def turn(key, h):
-            bank = psum.tile([P, 2, 2, P], F32, name="xt", tag="xt")
+            b = bank(("xt", key, h), [P, 2, 2, P])
             words = natural[key][:].bitcast(F32)
             for jj in range(2):
                 base = 256 * (2 * h + jj)
                 for u in range(2):
-                    nc.tensor.transpose(bank[:, jj, u, :], words[:, base + u : base + 256 : 2], ident[:])
-            xt_bank[key, h] = bank
+                    nc.tensor.transpose(b[:, jj, u, :], words[:, base + u : base + 256 : 2], ident[:])
 
-        def turn_out(key, h):
+        def turn_out(key, h, vec=False):
             if h == 0:
                 inter[key] = work.tile([P, 4 * D], BF16, name="inter", tag="inter", align_bytes=64)
-            dst = inter[key][:, 1024 * h : 1024 * (h + 1)].bitcast(F32)
-            nc.scalar.copy(
-                out=dst.rearrange("p (j r u) -> p j r u", j=2, u=2),
-                in_=xt_bank[key, h][:].rearrange("p j u r -> p j r u"),
-            )
+            dst = inter[key][:, 1024 * h : 1024 * (h + 1)].bitcast(F32).rearrange("p (j r u) -> p j r u", j=2, u=2)
+            src = banks["xt", key, h][:].rearrange("p j u r -> p j r u")
+            if vec:
+                nc.vector.tensor_copy(out=dst, in_=src)
+            else:
+                nc.scalar.copy(out=dst, in_=src)
 
         def quantize(key, src, pool, tag):
             codes[key] = pool.tile([P, D], U32, name="c_" + tag, tag="c_" + tag, align_bytes=64)
@@ -121,68 +140,84 @@ def tile_patchedsparsenetwork_pa_t_kernel(tc, x_bytes, x_scale, W0, b0, m0, W1, 
                 stop=True,
             )
 
-        h_bank, h_sb = {}, {}
+        planes, h_sb, y_sb, o_sb = {}, {}, {}, {}
 
-        def layer1(g, j):
-            bank = psum.tile([P, 4, P], F32, name="hb", tag="hb")
-            for t in range(4):
-                mm(bank[:, t, :], "W0", slice(P * t, P * (t + 1)), g, slice(P * j, P * (j + 1)))
-            h_bank[g, j] = bank
+        def layer1(g, t):
+            b = bank(("h", g, t), [P, GROUP])
+            mm(b[:], "W0", slice(P * t, P * (t + 1)), g, slice(0, GROUP))
 
-        def bias1(g, j):
-            if j == 0:
-                h_sb[g] = work.tile([P, 4 * D], BF16, name="h_sb", tag="h_sb", align_bytes=64)
-            dst = h_sb[g][:, j * D : (j + 1) * D].rearrange("p (n t) -> p n t", t=4)
-            nc.vector.tensor_tensor(out=dst, in0=h_bank[g, j][:].rearrange("p t n -> p n t"), in1=b0t[:], op=ALU.add)
-
-        h_planes = {}
-
-        def bias_relu1(g, j):
-            h_planes[g] = work.tile([P, 4, P], BF16, name="h_pl", tag="h_pl", align_bytes=64)
-            for t in range(4):
-                nc.scalar.activation(
-                    out=h_planes[g][:, t, :], in_=h_bank[g, j][:, t, :], func=ACT.Relu, bias=b0f[:, t : t + 1]
-                )
-
-        def interleave1(g, j):
-            dst = h_sb[g][:, j * D : (j + 1) * D].rearrange("p (n t) -> p n t", t=4)
-            nc.vector.tensor_copy(out=dst, in_=h_planes[g][:].rearrange("p t n -> p n t"))
-
-        def relu1(g):
-            nc.vector.tensor_scalar_max(h_sb[g][:, 0 : 3 * D], h_sb[g][:, 0 : 3 * D], 0.0)
-
-        o_bank, y_sb, t_bank, o_sb = {}, {}, {}, {}
-
-        def layer2(g, t):
-            bank = psum.tile([P, GROUP], F32, name="ob", tag="ob")
-            mm(bank[:], "W1", slice(P * t, P * (t + 1)), ("h", g), slice(0, GROUP))
-            o_bank[g, t] = bank
-
-        def bias2(g, t, vec):
+        def hidden(g, t, vec=False):
             if t == 0:
-                y_sb[g] = work.tile([P, 4, GROUP], F32, name="y_sb", tag="y_sb", align_bytes=64)
+                planes[g] = work.tile([P, 4, GROUP], BF16, name="planes", tag="planes", align_bytes=64)
+            b = banks["h", g, t]
             if vec:
                 nc.vector.tensor_scalar(
-                    out=y_sb[g][:, t, :], in0=o_bank[g, t][:], scalar1=b1f[:, t : t + 1], scalar2=0.0, op0=ALU.add, op1=ALU.max
+                    out=planes[g][:, t, :], in0=b[:], scalar1=b0f[:, t : t + 1], scalar2=0.0, op0=ALU.add, op1=ALU.max
                 )
             else:
-                nc.scalar.activation(out=y_sb[g][:, t, :], in_=o_bank[g, t][:], func=ACT.Relu, bias=b1f[:, t : t + 1])
+                nc.scalar.activation(out=planes[g][:, t, :], in_=b[:], func=ACT.Relu, bias=b0f[:, t : t + 1])
 
-        def back(g, j):
-            bank = psum.tile([P, 4, P], F32, name="tb", tag="tb")
-            for t in range(4):
-                nc.tensor.transpose(bank[:, t, :], y_sb[g][:, t, P * j : P * (j + 1)], ident[:])
-            t_bank[g, j] = bank
+        def interleave(g):
+            h_sb[g] = work.tile([P, 4 * D], BF16, name="h_sb", tag="h_sb", align_bytes=64)
+            dst = h_sb[g][:].rearrange("p (n t) -> p n t", t=4)
+            nc.vector.tensor_copy(out=dst, in_=planes[g][:].rearrange("p t n -> p n t"))
 
-        def back_out(g, j, vec):
-            if j == 0:
+        def layer2_ch(g, e):
+            b = bank(("y", g, e), [P, GROUP])
+            mm(b[:], "W1", slice(P * e, P * (e + 1)), ("h", g), slice(0, GROUP))
+
+        def bias_ch(g, e, vec=False):
+            if e == 0:
+                y_sb[g] = work.tile([P, 2, GROUP], F32, name="y_sb", tag="y_sb", align_bytes=64)
+            b = banks["y", g, e]
+            if vec:
+                nc.vector.tensor_scalar(
+                    out=y_sb[g][:, e, :], in0=b[:], scalar1=b1f[:, e : e + 1], scalar2=0.0, op0=ALU.add, op1=ALU.max
+                )
+            else:
+                nc.scalar.activation(out=y_sb[g][:, e, :], in_=b[:], func=ACT.Relu, bias=b1f[:, e : e + 1])
+
+        def back(g, h):
+            b = bank(("t", g, h), [P, 2, 2, P])
+            for jj in range(2):
+                j = 2 * h + jj
+                for e in range(2):
+                    nc.tensor.transpose(b[:, jj, e, :], y_sb[g][:, e, P * j : P * (j + 1)], ident[:])
+
+        def out_tile(g):
+            if g not in o_sb:
                 o_sb[g] = work.tile([P, 4, D], F32, name="o_sb", tag="o_sb", align_bytes=64)
-            dst = o_sb[g][:, j, :].rearrange("p (c t) -> p c t", t=4)
-            src = t_bank[g, j][:].rearrange("p t c -> p c t")
+            return o_sb[g]
+
+        def back_out(g, h, vec=False):
+            o = out_tile(g)
+            dst = o[:, 2 * h : 2 * h + 2, 0:HALF].rearrange("p j (m e) -> p j m e", e=2)
+            src = banks["t", g, h][:].rearrange("p j e m -> p j m e")
             if vec:
                 nc.vector.tensor_copy(out=dst, in_=src)
             else:
                 nc.scalar.copy(out=dst, in_=src)
+
+        def layer2_tok(g, h):
+            b = bank(("o", g, h), [P, 2, HALF])
+            for jj in range(2):
+                j = 2 * h + jj
+                mm(b[:, jj, :], ("h", g), slice(P * j, P * (j + 1)), "W1", slice(HALF, D))
+
+        def bias_tok(g, h):
+            o = out_tile(g)
+            nc.vector.tensor_tensor(
+                out=o[:, 2 * h : 2 * h + 2, HALF:D], in0=banks["o", g, h][:], in1=b1t[:], op=ALU.add
+            )
+
+        def relu_tok(g, eng, j0=0, j1=4):
+            v = o_sb[g][:, j0:j1, HALF:D]
+            if eng == "V":
+                nc.vector.tensor_scalar_max(v, v, 0.0)
+            elif eng == "G":
+                nc.gpsimd.tensor_scalar(out=v, in0=v, scalar1=0.0, scalar2=0.0, op0=ALU.max, op1=ALU.add)
+            else:
+                nc.scalar.activation(out=v, in_=v, func=ACT.Relu)
 
         def store(g, j0, j1):
             rows = out[g * GROUP : (g + 1) * GROUP, :].rearrange("(r j) c -> r j c", j=4)
@@ -191,93 +226,93 @@ def tile_patchedsparsenetwork_pa_t_kernel(tc, x_bytes, x_scale, W0, b0, m0, W1, 
         def ok(g):
             return 0 <= g < NG
 
+        for j in range(4):
+            widen_block(0, j)
+            if j % 2 == 1:
+                turn(0, j // 2)
+                turn_out(0, j // 2)
         mask_w("W0", "w0", "m0")
         for h in range(2):
             turn("W0", h)
             turn_out("W0", h)
-        widen(0, 0)
-        widen(0, 1)
-        for h in range(2):
-            turn(0, h)
-            turn_out(0, h)
-        quantize("W0", inter["W0"], keep, "w0")
-        widen(1, 0)
         quantize(0, inter[0], work, "x")
-        layer1(0, 0)
-        layer1(0, 1)
+        widen(1, 0)
+        quantize("W0", inter["W0"], keep, "w0")
+        for t in range(4):
+            layer1(0, t)
         widen(1, 1)
         mask_w("W1", "w1", "m1")
-        for h in range(2):
-            turn("W1", h)
-            turn_out("W1", h)
 
-        for i in range(NG + 2):
+        for i in range(NG + 1):
             cur, nxt, nx2, prv, pp = ok(i), ok(i + 1), ok(i + 2), ok(i - 1), ok(i - 2)
-            tail = i >= NG
+            last = i >= NG - 1
             if nxt:
                 turn(i + 1, 0)
-            if pp:
-                back(i - 2, 0)
-            if nxt:
-                turn_out(i + 1, 0)
-            if pp:
-                back_out(i - 2, 0, tail)
-            if cur:
-                bias1(i, 0)
-            if prv:
-                layer2(i - 1, 0)
-                layer2(i - 1, 1)
-            if cur:
-                layer1(i, 2)
-                bias1(i, 1)
+                turn(i + 1, 1)
             if nx2:
                 widen(i + 2, 0)
+                widen(i + 2, 1)
             if prv:
-                bias2(i - 1, 0, False)
+                layer2_tok(i - 1, 0)
+                layer2_tok(i - 1, 1)
+                layer2_ch(i - 1, 0)
+                layer2_ch(i - 1, 1)
+                if i < NG:
+                    bias_tok(i - 1, 0)
+                    bias_tok(i - 1, 1)
+            if cur:
+                hidden(i, 0)
+                hidden(i, 1, last)
             if nxt:
-                turn(i + 1, 1)
-            if pp:
-                back(i - 2, 1)
-            if nxt:
+                turn_out(i + 1, 0)
                 turn_out(i + 1, 1)
-            if prv:
-                bias2(i - 1, 1, tail)
-            if pp:
-                back_out(i - 2, 1, False)
             if cur:
-                layer1(i, 3)
-                bias_relu1(i, 3)
-            if prv:
-                layer2(i - 1, 2)
-                layer2(i - 1, 3)
-            if cur:
-                bias1(i, 2)
-            if prv:
-                bias2(i - 1, 2, False)
-                bias2(i - 1, 3, tail)
-            if pp:
-                back(i - 2, 2)
-                back(i - 2, 3)
+                hidden(i, 2)
+                hidden(i, 3, i >= NG - 2)
             if i == 0:
-                quantize("W1", inter["W1"], keep, "w1")
+                for h in range(2):
+                    turn("W1", h)
+                    turn_out("W1", h)
             if nxt:
                 quantize(i + 1, inter[i + 1], work, "x")
+            if pp and i < NG:
+                back(i - 2, 0)
+                back(i - 2, 1)
+                back_out(i - 2, 0)
+                back_out(i - 2, 1)
+                store(i - 2, 0, 4)
+            if prv and i < NG:
+                bias_ch(i - 1, 0)
+                bias_ch(i - 1, 1)
+                if i < NG - 2:
+                    relu_tok(i - 1, "S", 2, 4)
             if cur:
-                relu1(i)
-                interleave1(i, 3)
-            if nx2:
-                widen(i + 2, 1)
+                interleave(i)
+            if i == 0:
+                quantize("W1", inter["W1"], keep, "w1")
+            if prv and i < NG:
+                relu_tok(i - 1, "V", 0, 2 if i < NG - 2 else 4)
             if cur:
                 quantize(("h", i), h_sb[i], work, "h")
-            if pp:
-                back_out(i - 2, 2, tail)
-                back_out(i - 2, 3, False)
             if nxt:
-                layer1(i + 1, 0)
-                layer1(i + 1, 1)
-            if pp:
-                if tail:
-                    store(i - 2, 0, 2)
-                    store(i - 2, 2, 4)
-                else:
-                    store(i - 2, 0, 4)
+                for t in range(4):
+                    layer1(i + 1, t)
+            if i == NG - 1:
+                back(i - 1, 0)
+                back(i - 1, 1)
+                back_out(i - 1, 0)
+                back_out(i - 1, 1, True)
+                store(i - 1, 0, 4)
+        g = NG - 1
+        bias_ch(g, 0)
+        bias_ch(g, 1, True)
+        bias_tok(g, 0)
+        back(g, 0)
+        relu_tok(g, "S", 0, 2)
+        bias_tok(g, 1)
+        back(g, 1)
+        back_out(g, 0)
+        store(g, 0, 2)
+        relu_tok(g, "V", 2, 4)
+        back_out(g, 1, True)
+        store(g, 2, 4)

@@ -28,17 +28,15 @@ def tile_patchedsparsenetwork_pa_t_kernel(tc, x_bytes, x_scale, W0, b0, m0, W1, 
         psum = ctx.enter_context(tc.psum_pool(name="psum", bufs=8))
         ctx.enter_context(tc.manual_schedule())
 
-        scale = keep.tile([P, 2 * D], F32, name="scale", align_bytes=64)
-        nc.scalar.dma_start(out=scale[:, 0:D], in_=x_scale.rearrange("o k -> (o k)").partition_broadcast(P))
+        scale_col = keep.tile([P, 4], F32, name="scale_col", align_bytes=64)
+        nc.scalar.dma_start(out=scale_col[:], in_=x_scale.rearrange("o (n m) -> (o n) m", m=4))
         warm = keep.tile([P, 1], F32, name="warm", align_bytes=64)
         nc.vector.memset(warm[:], 0.0)
         nc.scalar.activation(out=warm[:], in_=warm[:], func=ACT.Relu)
         b0h = keep.tile([P, 4], BF16, name="b0h", align_bytes=64)
         nc.scalar.dma_start(out=b0h[:], in_=b0.rearrange("(p t) -> p t", t=4))
-        b1h = keep.tile([P, 2], BF16, name="b1h", align_bytes=64)
-        nc.scalar.dma_start(out=b1h[:], in_=b1[0:HALF].rearrange("(m e) -> m e", e=2))
-        b1w = keep.tile([P, HALF], BF16, name="b1w", align_bytes=64)
-        nc.scalar.dma_start(out=b1w[:], in_=b1[HALF:D].partition_broadcast(P))
+        b1h = keep.tile([P, 2, 2], BF16, name="b1h", align_bytes=64)
+        nc.scalar.dma_start(out=b1h[:], in_=b1.rearrange("(h n m) -> n h m", h=2, m=2))
 
         raw = {}
 
@@ -70,13 +68,13 @@ def tile_patchedsparsenetwork_pa_t_kernel(tc, x_bytes, x_scale, W0, b0, m0, W1, 
 
         ident = keep.tile([P, P], F32, name="ident", align_bytes=64)
         make_identity(nc, ident[:])
-        nc.scalar.copy(out=scale[:, D : 2 * D], in_=scale[:, 0:D])
         b0f = keep.tile([P, 4], F32, name="b0f", align_bytes=64)
         nc.scalar.copy(out=b0f[:], in_=b0h[:])
-        b1f = keep.tile([P, 2], F32, name="b1f", align_bytes=64)
-        nc.scalar.copy(out=b1f[:], in_=b1h[:])
+        b1f2 = keep.tile([P, 2, 2], F32, name="b1f2", align_bytes=64)
+        nc.scalar.copy(out=b1f2[:], in_=b1h[:])
+        b1f = b1f2[:, 0, :]
+        scale = keep.tile([P, 4, D], F32, name="scale", align_bytes=64)
         b1t = keep.tile([P, 2, HALF], F32, name="b1t", align_bytes=64)
-        nc.scalar.copy(out=b1t[:], in_=b1w[:].unsqueeze(1).to_broadcast([P, 2, HALF]))
 
         natural, inter, codes, scales = {}, {}, {}, {}
         banks = {}
@@ -84,6 +82,22 @@ def tile_patchedsparsenetwork_pa_t_kernel(tc, x_bytes, x_scale, W0, b0, m0, W1, 
         def bank(key, shape):
             banks[key] = psum.tile(shape, F32, name="bank", tag="bank")
             return banks[key]
+
+        def spread_scale():
+            b = bank("scale", [P, 4, P])
+            for m in range(4):
+                nc.tensor.transpose(b[:, m, :], scale_col[:, m : m + 1].to_broadcast([P, P]), ident[:])
+            src = b[:].rearrange("p m n -> p n m")
+            for j in range(4):
+                nc.scalar.copy(out=scale[:, j, :].rearrange("p (n m) -> p n m", m=4), in_=src)
+
+        def spread_b1():
+            b = bank("b1", [P, 2, P])
+            for m in range(2):
+                nc.tensor.transpose(b[:, m, :], b1f2[:, 1, m : m + 1].to_broadcast([P, P]), ident[:])
+            src = b[:].rearrange("p m n -> p n m")
+            for j in range(2):
+                nc.scalar.copy(out=b1t[:, j, :].rearrange("p (n m) -> p n m", m=2), in_=src)
 
         def new_natural(key):
             natural[key] = work.tile([P, 4 * D], BF16, name="nat", tag="nat", align_bytes=64)
@@ -94,17 +108,17 @@ def tile_patchedsparsenetwork_pa_t_kernel(tc, x_bytes, x_scale, W0, b0, m0, W1, 
                 out=natural[key][:].rearrange("p (t k) -> p t k", t=4), in0=raw[w][:], in1=raw[m][:], op=ALU.mult
             )
 
-        def widen(g, h):
-            if h == 0:
-                new_natural(g)
-            c = slice(2 * h * D, 2 * (h + 1) * D)
-            nc.vector.tensor_tensor(out=natural[g][:, c], in0=x8[g][:, c].bitcast(F8), in1=scale[:], op=ALU.mult)
+        def widen(g):
+            new_natural(g)
+            nc.vector.tensor_tensor(
+                out=natural[g][:], in0=x8[g][:].bitcast(F8), in1=scale[:].rearrange("p j k -> p (j k)"), op=ALU.mult
+            )
 
         def widen_block(g, j):
             if j == 0:
                 new_natural(g)
             c = slice(j * D, (j + 1) * D)
-            nc.vector.tensor_tensor(out=natural[g][:, c], in0=x8[g][:, c].bitcast(F8), in1=scale[:, 0:D], op=ALU.mult)
+            nc.vector.tensor_tensor(out=natural[g][:, c], in0=x8[g][:, c].bitcast(F8), in1=scale[:, 0, :], op=ALU.mult)
 
         def turn(key, h):
             b = bank(("xt", key, h), [P, 2, 2, P])
@@ -159,8 +173,8 @@ def tile_patchedsparsenetwork_pa_t_kernel(tc, x_bytes, x_scale, W0, b0, m0, W1, 
 
         def interleave(g):
             h_sb[g] = work.tile([P, 4 * D], BF16, name="h_sb", tag="h_sb", align_bytes=64)
-            dst = h_sb[g][:].rearrange("p (n t) -> p n t", t=4)
-            nc.vector.tensor_copy(out=dst, in_=planes[g][:].rearrange("p t n -> p n t"))
+            dst = h_sb[g][:].rearrange("p (c i t) -> p c t i", i=4, t=4)
+            nc.vector.tensor_copy(out=dst, in_=planes[g][:].rearrange("p t (c i) -> p c t i", i=4))
 
         def layer2_ch(g, e):
             b = bank(("y", g, e), [P, GROUP])
@@ -226,6 +240,7 @@ def tile_patchedsparsenetwork_pa_t_kernel(tc, x_bytes, x_scale, W0, b0, m0, W1, 
         def ok(g):
             return 0 <= g < NG
 
+        spread_scale()
         for j in range(4):
             widen_block(0, j)
             if j % 2 == 1:
@@ -235,78 +250,84 @@ def tile_patchedsparsenetwork_pa_t_kernel(tc, x_bytes, x_scale, W0, b0, m0, W1, 
         for h in range(2):
             turn("W0", h)
             turn_out("W0", h)
+        widen(1)
         quantize(0, inter[0], work, "x")
-        widen(1, 0)
         quantize("W0", inter["W0"], keep, "w0")
-        for t in range(4):
+        turn(1, 0)
+        turn(1, 1)
+        for t in range(3):
             layer1(0, t)
-        widen(1, 1)
         mask_w("W1", "w1", "m1")
 
-        for i in range(NG + 1):
+        for i in range(NG):
             cur, nxt, nx2, prv, pp = ok(i), ok(i + 1), ok(i + 2), ok(i - 1), ok(i - 2)
-            last = i >= NG - 1
-            if nxt:
-                turn(i + 1, 0)
-                turn(i + 1, 1)
-            if nx2:
-                widen(i + 2, 0)
-                widen(i + 2, 1)
+            drain = i >= NG - 2
             if prv:
                 layer2_tok(i - 1, 0)
+            layer1(i, 3)
+            if prv:
                 layer2_tok(i - 1, 1)
-                layer2_ch(i - 1, 0)
-                layer2_ch(i - 1, 1)
-                if i < NG:
-                    bias_tok(i - 1, 0)
-                    bias_tok(i - 1, 1)
-            if cur:
-                hidden(i, 0)
-                hidden(i, 1, last)
             if nxt:
                 turn_out(i + 1, 0)
                 turn_out(i + 1, 1)
-            if cur:
-                hidden(i, 2)
-                hidden(i, 3, i >= NG - 2)
+            if nx2:
+                widen(i + 2)
+            hidden(i, 0)
+            hidden(i, 1, i == NG - 1)
+            if i == 0:
+                spread_b1()
+            hidden(i, 2)
+            hidden(i, 3, drain)
+            if nxt:
+                quantize(i + 1, inter[i + 1], work, "x")
+            if prv:
+                bias_tok(i - 1, 0)
+                bias_tok(i - 1, 1)
             if i == 0:
                 for h in range(2):
                     turn("W1", h)
                     turn_out("W1", h)
-            if nxt:
-                quantize(i + 1, inter[i + 1], work, "x")
-            if pp and i < NG:
+            interleave(i)
+            if i == 0:
+                quantize("W1", inter["W1"], keep, "w1")
+            sfull = False
+            if prv and not (sfull and not drain):
+                relu_tok(i - 1, "V", 0, 4 if drain else 2)
+            quantize(("h", i), h_sb[i], work, "h")
+            if pp:
                 back(i - 2, 0)
                 back(i - 2, 1)
+            if prv:
+                layer2_ch(i - 1, 0)
+                layer2_ch(i - 1, 1)
+            if pp:
                 back_out(i - 2, 0)
                 back_out(i - 2, 1)
                 store(i - 2, 0, 4)
-            if prv and i < NG:
+            if prv:
                 bias_ch(i - 1, 0)
                 bias_ch(i - 1, 1)
-                if i < NG - 2:
-                    relu_tok(i - 1, "S", 2, 4)
-            if cur:
-                interleave(i)
-            if i == 0:
-                quantize("W1", inter["W1"], keep, "w1")
-            if prv and i < NG:
-                relu_tok(i - 1, "V", 0, 2 if i < NG - 2 else 4)
-            if cur:
-                quantize(("h", i), h_sb[i], work, "h")
+                if not drain:
+                    relu_tok(i - 1, "S", 0 if sfull else 2, 4)
+            if nx2:
+                turn(i + 2, 0)
+                turn(i + 2, 1)
             if nxt:
-                for t in range(4):
+                for t in range(3):
                     layer1(i + 1, t)
-            if i == NG - 1:
-                back(i - 1, 0)
-                back(i - 1, 1)
-                back_out(i - 1, 0)
-                back_out(i - 1, 1, True)
-                store(i - 1, 0, 4)
         g = NG - 1
+        back(g - 1, 0)
+        back(g - 1, 1)
+        layer2_tok(g, 0)
+        layer2_ch(g, 0)
+        layer2_ch(g, 1)
+        layer2_tok(g, 1)
+        back_out(g - 1, 0)
+        back_out(g - 1, 1, True)
+        store(g - 1, 0, 4)
+        bias_tok(g, 0)
         bias_ch(g, 0)
         bias_ch(g, 1, True)
-        bias_tok(g, 0)
         back(g, 0)
         relu_tok(g, "S", 0, 2)
         bias_tok(g, 1)

@@ -102,11 +102,12 @@ def tile_patchedsparsenetwork_pa_t_kernel(tc, x_bytes, x_scale, W0, b0, m0, W1, 
         def new_natural(key):
             natural[key] = work.tile([P, 4 * D], BF16, name="nat", tag="nat", align_bytes=64)
 
-        def mask_w(key, w, m):
-            new_natural(key)
-            nc.vector.tensor_tensor(
-                out=natural[key][:].rearrange("p (t k) -> p t k", t=4), in0=raw[w][:], in1=raw[m][:], op=ALU.mult
-            )
+        def mask_w(key, w, m, h):
+            if h == 0:
+                new_natural(key)
+            t = slice(2 * h, 2 * h + 2)
+            dst = natural[key][:].rearrange("p (t k) -> p t k", t=4)[:, t, :]
+            nc.vector.tensor_tensor(out=dst, in0=raw[w][:, t, :], in1=raw[m][:, t, :], op=ALU.mult)
 
         def widen(g):
             new_natural(g)
@@ -154,7 +155,7 @@ def tile_patchedsparsenetwork_pa_t_kernel(tc, x_bytes, x_scale, W0, b0, m0, W1, 
                 stop=True,
             )
 
-        planes, h_sb, y_sb, o_sb = {}, {}, {}, {}
+        planes, h_sb, y_sb, o_ch, o_tok = {}, {}, {}, {}, {}
 
         def layer1(g, t):
             b = bank(("h", g, t), [P, GROUP])
@@ -198,14 +199,11 @@ def tile_patchedsparsenetwork_pa_t_kernel(tc, x_bytes, x_scale, W0, b0, m0, W1, 
                 for e in range(2):
                     nc.tensor.transpose(b[:, jj, e, :], y_sb[g][:, e, P * j : P * (j + 1)], ident[:])
 
-        def out_tile(g):
-            if g not in o_sb:
-                o_sb[g] = work.tile([P, 4, D], F32, name="o_sb", tag="o_sb", align_bytes=64)
-            return o_sb[g]
 
         def back_out(g, h, vec=False):
-            o = out_tile(g)
-            dst = o[:, 2 * h : 2 * h + 2, 0:HALF].rearrange("p j (m e) -> p j m e", e=2)
+            if h == 0:
+                o_ch[g] = work.tile([P, 4, HALF], F32, name="o_ch", tag="o_ch", align_bytes=64)
+            dst = o_ch[g][:, 2 * h : 2 * h + 2, :].rearrange("p j (m e) -> p j m e", e=2)
             src = banks["t", g, h][:].rearrange("p j e m -> p j m e")
             if vec:
                 nc.vector.tensor_copy(out=dst, in_=src)
@@ -219,13 +217,14 @@ def tile_patchedsparsenetwork_pa_t_kernel(tc, x_bytes, x_scale, W0, b0, m0, W1, 
                 mm(b[:, jj, :], ("h", g), slice(P * j, P * (j + 1)), "W1", slice(HALF, D))
 
         def bias_tok(g, h):
-            o = out_tile(g)
+            if h == 0:
+                o_tok[g] = work.tile([P, 4, HALF], F32, name="o_tok", tag="o_tok", align_bytes=64)
             nc.vector.tensor_tensor(
-                out=o[:, 2 * h : 2 * h + 2, HALF:D], in0=banks["o", g, h][:], in1=b1t[:], op=ALU.add
+                out=o_tok[g][:, 2 * h : 2 * h + 2, :], in0=banks["o", g, h][:], in1=b1t[:], op=ALU.add
             )
 
         def relu_tok(g, eng, j0=0, j1=4):
-            v = o_sb[g][:, j0:j1, HALF:D]
+            v = o_tok[g][:, j0:j1, :]
             if eng == "V":
                 nc.vector.tensor_scalar_max(v, v, 0.0)
             elif eng == "G":
@@ -233,55 +232,63 @@ def tile_patchedsparsenetwork_pa_t_kernel(tc, x_bytes, x_scale, W0, b0, m0, W1, 
             else:
                 nc.scalar.activation(out=v, in_=v, func=ACT.Relu)
 
-        def store(g, j0, j1):
+        def store(g, tok, j0=0, j1=4):
             rows = out[g * GROUP : (g + 1) * GROUP, :].rearrange("(r j) c -> r j c", j=4)
-            nc.sync.dma_start(out=rows[:, j0:j1, :], in_=o_sb[g][:, j0:j1, :])
+            if tok:
+                nc.sync.dma_start(out=rows[:, j0:j1, HALF:D], in_=o_tok[g][:, j0:j1, :])
+            else:
+                nc.sync.dma_start(out=rows[:, j0:j1, 0:HALF], in_=o_ch[g][:, j0:j1, :])
 
         def ok(g):
             return 0 <= g < NG
 
+        on_vector = [(NG - 1, 3)]
         spread_scale()
         for j in range(4):
             widen_block(0, j)
             if j % 2 == 1:
                 turn(0, j // 2)
                 turn_out(0, j // 2)
-        mask_w("W0", "w0", "m0")
         for h in range(2):
+            mask_w("W0", "w0", "m0", h)
             turn("W0", h)
             turn_out("W0", h)
-        widen(1)
+        widen_block(1, 0)
+        widen_block(1, 1)
         quantize(0, inter[0], work, "x")
         quantize("W0", inter["W0"], keep, "w0")
-        turn(1, 0)
-        turn(1, 1)
+        widen_block(1, 2)
+        widen_block(1, 3)
         for t in range(3):
             layer1(0, t)
-        mask_w("W1", "w1", "m1")
+        turn(1, 0)
+        turn(1, 1)
+        for h in range(2):
+            mask_w("W1", "w1", "m1", h)
 
         for i in range(NG):
             cur, nxt, nx2, prv, pp = ok(i), ok(i + 1), ok(i + 2), ok(i - 1), ok(i - 2)
-            drain = i >= NG - 2
             if prv:
                 layer2_tok(i - 1, 0)
             layer1(i, 3)
             if prv:
                 layer2_tok(i - 1, 1)
+            if nx2:
+                widen(i + 2)
+            hidden(i, 0, (i, 0) in on_vector)
+            hidden(i, 1, (i, 1) in on_vector)
             if nxt:
                 turn_out(i + 1, 0)
                 turn_out(i + 1, 1)
-            if nx2:
-                widen(i + 2)
-            hidden(i, 0)
-            hidden(i, 1, i == NG - 1)
             if i == 0:
                 spread_b1()
-            hidden(i, 2)
-            hidden(i, 3, drain)
+            hidden(i, 2, (i, 2) in on_vector)
+            hidden(i, 3, (i, 3) in on_vector)
+            if prv:
+                bias_tok(i - 1, 0)
             if nxt:
                 quantize(i + 1, inter[i + 1], work, "x")
             if prv:
-                bias_tok(i - 1, 0)
                 bias_tok(i - 1, 1)
             if i == 0:
                 for h in range(2):
@@ -290,9 +297,9 @@ def tile_patchedsparsenetwork_pa_t_kernel(tc, x_bytes, x_scale, W0, b0, m0, W1, 
             interleave(i)
             if i == 0:
                 quantize("W1", inter["W1"], keep, "w1")
-            sfull = False
-            if prv and not (sfull and not drain):
-                relu_tok(i - 1, "V", 0, 4 if drain else 2)
+            split = 4 if i == NG - 2 else 2 if i == NG - 1 else 2
+            if prv:
+                relu_tok(i - 1, "V", 0, split)
             quantize(("h", i), h_sb[i], work, "h")
             if pp:
                 back(i - 2, 0)
@@ -303,12 +310,13 @@ def tile_patchedsparsenetwork_pa_t_kernel(tc, x_bytes, x_scale, W0, b0, m0, W1, 
             if pp:
                 back_out(i - 2, 0)
                 back_out(i - 2, 1)
-                store(i - 2, 0, 4)
+                store(i - 2, False)
             if prv:
                 bias_ch(i - 1, 0)
                 bias_ch(i - 1, 1)
-                if not drain:
-                    relu_tok(i - 1, "S", 0 if sfull else 2, 4)
+                if split < 4:
+                    relu_tok(i - 1, "S", split, 4)
+                store(i - 1, True)
             if nx2:
                 turn(i + 2, 0)
                 turn(i + 2, 1)
@@ -323,17 +331,19 @@ def tile_patchedsparsenetwork_pa_t_kernel(tc, x_bytes, x_scale, W0, b0, m0, W1, 
         layer2_ch(g, 1)
         layer2_tok(g, 1)
         back_out(g - 1, 0)
-        back_out(g - 1, 1, True)
-        store(g - 1, 0, 4)
+        back_out(g - 1, 1, False)
+        store(g - 1, False)
         bias_tok(g, 0)
         bias_ch(g, 0)
         bias_ch(g, 1, True)
         back(g, 0)
         relu_tok(g, "S", 0, 2)
+        store(g, True, 0, 2)
         bias_tok(g, 1)
         back(g, 1)
         back_out(g, 0)
-        store(g, 0, 2)
+        store(g, False, 0, 2)
         relu_tok(g, "V", 2, 4)
+        store(g, True, 2, 4)
         back_out(g, 1, True)
-        store(g, 2, 4)
+        store(g, False, 2, 4)

@@ -7,17 +7,27 @@ F32 = mybir.dt.float32
 BF16 = mybir.dt.bfloat16
 U32 = mybir.dt.uint32
 U8 = mybir.dt.uint8
-F8 = mybir.dt.float8_e4m3fn
-FP8X4 = mybir.dt.float8_e4m3fn_x4
+E4M3FN = mybir.dt.float8_e4m3fn
+E4M3FN_X4 = mybir.dt.float8_e4m3fn_x4
 ALU = mybir.AluOpType
 ACT = mybir.ActivationFunctionType
 
 P = 128
-B, D = 8192, 512
-HALF = D // 2
-GROUP = 512
-NG = B // GROUP
-FLOPS = 2 * B * D * D * 2
+PACK = 4
+SETS = 4
+K = 512
+HALF = K // 2
+N_TOKENS = 8192
+GROUP = SETS * P
+N_GROUPS = N_TOKENS // GROUP
+
+FLOPS = 2 * (2 * N_TOKENS * K * K)
+
+
+def sets_with_relu_on_vector(g):
+    if g == N_GROUPS - 3:
+        return 4
+    return 3 if g % 4 == 3 and g < N_GROUPS - 3 else 2
 
 
 def tile_patchedsparsenetwork_pa_t_kernel(tc, x_bytes, x_scale, W0, b0, m0, W1, b1, m1, out):
@@ -28,55 +38,57 @@ def tile_patchedsparsenetwork_pa_t_kernel(tc, x_bytes, x_scale, W0, b0, m0, W1, 
         psum = ctx.enter_context(tc.psum_pool(name="psum", bufs=8))
         ctx.enter_context(tc.manual_schedule())
 
-        scale_col = keep.tile([P, 4], F32, name="scale_col", align_bytes=64)
-        nc.scalar.dma_start(out=scale_col[:], in_=x_scale.rearrange("o (n m) -> (o n) m", m=4))
+        scale_cols = keep.tile([P, PACK], F32, name="scale_cols", align_bytes=64)
+        nc.scalar.dma_start(out=scale_cols[:], in_=x_scale.rearrange("o (n m) -> (o n) m", m=PACK))
         warm = keep.tile([P, 1], F32, name="warm", align_bytes=64)
         nc.vector.memset(warm[:], 0.0)
         nc.scalar.activation(out=warm[:], in_=warm[:], func=ACT.Relu)
-        b0h = keep.tile([P, 4], BF16, name="b0h", align_bytes=64)
-        nc.scalar.dma_start(out=b0h[:], in_=b0.rearrange("(p t) -> p t", t=4))
-        b1h = keep.tile([P, 2, 2], BF16, name="b1h", align_bytes=64)
-        nc.scalar.dma_start(out=b1h[:], in_=b1.rearrange("(h n m) -> n h m", h=2, m=2))
+        b0_bf16 = keep.tile([P, PACK], BF16, name="b0_bf16", align_bytes=64)
+        nc.scalar.dma_start(out=b0_bf16[:], in_=b0.rearrange("(p t) -> p t", t=PACK))
+        b1_bf16 = keep.tile([P, 2, 2], BF16, name="b1_bf16", align_bytes=64)
+        nc.scalar.dma_start(out=b1_bf16[:], in_=b1.rearrange("(h m e) -> m h e", h=2, e=2))
 
-        raw = {}
+        w0_rows = keep.tile([P, SETS, K], BF16, name="w0_rows", align_bytes=64)
+        m0_rows = keep.tile([P, SETS, K], BF16, name="m0_rows", align_bytes=64)
+        w1_rows = keep.tile([P, SETS, K], BF16, name="w1_rows", align_bytes=64)
+        m1_rows = keep.tile([P, SETS, K], BF16, name="m1_rows", align_bytes=64)
 
-        def load_w(key, src, split):
-            t = keep.tile([P, 4, D], BF16, name=key, align_bytes=64)
-            if split:
-                nc.sync.dma_start(out=t[:, 0:2, :], in_=src[0:HALF, :].rearrange("(m e) k -> m e k", e=2))
-                nc.sync.dma_start(out=t[:, 2:4, :], in_=src[HALF:D, :].rearrange("(e m) k -> m e k", e=2))
-            else:
-                nc.sync.dma_start(out=t[:], in_=src.rearrange("(m t) k -> m t k", t=4))
-            raw[key] = t
+        def load_half(dst, src, half):
+            nc.sync.dma_start(out=dst[:, 2 * half : 2 * half + 2, :], in_=src)
+
+        def layer1_rows(w, half):
+            return w.rearrange("(m s) k -> m s k", s=SETS)[:, 2 * half : 2 * half + 2, :]
+
+        def layer2_rows(w, half):
+            part = w[half * HALF : (half + 1) * HALF, :]
+            return part.rearrange("(m s) k -> m s k", s=2) if half == 0 else part.rearrange("(s m) k -> m s k", s=2)
 
         x8 = {}
 
         def load_x(g):
-            t = keep.tile([P, 4 * D], U8, name="x8_%d" % g, align_bytes=64)
-            rows = x_bytes[g * GROUP : (g + 1) * GROUP, :]
-            nc.sync.dma_start(out=t[:], in_=rows.rearrange("(r j) k -> r (j k)", j=4))
-            x8[g] = t
+            x8[g] = keep.tile([P, SETS * K], U8, name="x8_%d" % g, align_bytes=64)
+            tokens = x_bytes[g * GROUP : (g + 1) * GROUP, :]
+            nc.sync.dma_start(out=x8[g][:], in_=tokens.rearrange("(r j) k -> r (j k)", j=SETS))
 
+        for half in range(2):
+            load_half(w0_rows, layer1_rows(W0, half), half)
+            load_half(m0_rows, layer1_rows(m0, half), half)
         load_x(0)
-        load_w("w0", W0, False)
-        load_w("m0", m0, False)
         load_x(1)
-        load_w("w1", W1, True)
-        load_w("m1", m1, True)
-        for g in range(2, NG):
+        for half in range(2):
+            load_half(w1_rows, layer2_rows(W1, half), half)
+            load_half(m1_rows, layer2_rows(m1, half), half)
+        for g in range(2, N_GROUPS):
             load_x(g)
 
         ident = keep.tile([P, P], F32, name="ident", align_bytes=64)
         make_identity(nc, ident[:])
-        b0f = keep.tile([P, 4], F32, name="b0f", align_bytes=64)
-        nc.scalar.copy(out=b0f[:], in_=b0h[:])
-        b1f2 = keep.tile([P, 2, 2], F32, name="b1f2", align_bytes=64)
-        nc.scalar.copy(out=b1f2[:], in_=b1h[:])
-        b1f = b1f2[:, 0, :]
-        scale = keep.tile([P, 4, D], F32, name="scale", align_bytes=64)
-        b1t = keep.tile([P, 2, HALF], F32, name="b1t", align_bytes=64)
 
-        natural, inter, codes, scales = {}, {}, {}, {}
+        b0_cols = keep.tile([P, PACK], F32, name="b0_cols", align_bytes=64)
+        b1_cols = keep.tile([P, 2, 2], F32, name="b1_cols", align_bytes=64)
+        scale = keep.tile([P, SETS, K], F32, name="scale", align_bytes=64)
+        b1_spread = keep.tile([P, 2, HALF], F32, name="b1_spread", align_bytes=64)
+
         banks = {}
 
         def bank(key, shape):
@@ -84,266 +96,268 @@ def tile_patchedsparsenetwork_pa_t_kernel(tc, x_bytes, x_scale, W0, b0, m0, W1, 
             return banks[key]
 
         def spread_scale():
-            b = bank("scale", [P, 4, P])
-            for m in range(4):
-                nc.tensor.transpose(b[:, m, :], scale_col[:, m : m + 1].to_broadcast([P, P]), ident[:])
-            src = b[:].rearrange("p m n -> p n m")
-            for j in range(4):
-                nc.scalar.copy(out=scale[:, j, :].rearrange("p (n m) -> p n m", m=4), in_=src)
+            b = bank("scale", [P, PACK, P])
+            for m in range(PACK):
+                nc.tensor.transpose(b[:, m, :], scale_cols[:, m : m + 1].to_broadcast([P, P]), ident[:])
+            nc.scalar.copy(
+                out=scale[:, 0, :].rearrange("p (n m) -> p n m", m=PACK), in_=b[:].rearrange("p m n -> p n m")
+            )
+            nc.scalar.copy(out=scale[:, 1:SETS, :], in_=scale[:, 0:1, :].to_broadcast([P, SETS - 1, K]))
 
         def spread_b1():
             b = bank("b1", [P, 2, P])
-            for m in range(2):
-                nc.tensor.transpose(b[:, m, :], b1f2[:, 1, m : m + 1].to_broadcast([P, P]), ident[:])
-            src = b[:].rearrange("p m n -> p n m")
-            for j in range(2):
-                nc.scalar.copy(out=b1t[:, j, :].rearrange("p (n m) -> p n m", m=2), in_=src)
+            for e in range(2):
+                nc.tensor.transpose(b[:, e, :], b1_cols[:, 1, e : e + 1].to_broadcast([P, P]), ident[:])
+            for copy in range(2):
+                nc.scalar.copy(
+                    out=b1_spread[:, copy, :].rearrange("p (n e) -> p n e", e=2), in_=b[:].rearrange("p e n -> p n e")
+                )
 
-        def new_natural(key):
-            natural[key] = work.tile([P, 4 * D], BF16, name="nat", tag="nat", align_bytes=64)
+        plain, packed, codes, scale_bytes = {}, {}, {}, {}
 
-        def mask_w(key, w, m, h):
-            if h == 0:
-                new_natural(key)
-            t = slice(2 * h, 2 * h + 2)
-            dst = natural[key][:].rearrange("p (t k) -> p t k", t=4)[:, t, :]
-            nc.vector.tensor_tensor(out=dst, in0=raw[w][:, t, :], in1=raw[m][:, t, :], op=ALU.mult)
+        def new_plain(key):
+            plain[key] = work.tile([P, SETS * K], BF16, name="plain", tag="plain", align_bytes=64)
 
-        def widen(g):
-            new_natural(g)
+        def mask_half(key, w, m, half):
+            if half == 0:
+                new_plain(key)
+            sets = slice(2 * half, 2 * half + 2)
+            dst = plain[key][:].rearrange("p (s k) -> p s k", s=SETS)[:, sets, :]
+            nc.vector.tensor_tensor(out=dst, in0=w[:, sets, :], in1=m[:, sets, :], op=ALU.mult)
+
+        def widen_set(g, j):
+            if j == 0:
+                new_plain(g)
+            cols = slice(j * K, (j + 1) * K)
             nc.vector.tensor_tensor(
-                out=natural[g][:], in0=x8[g][:].bitcast(F8), in1=scale[:].rearrange("p j k -> p (j k)"), op=ALU.mult
+                out=plain[g][:, cols], in0=x8[g][:, cols].bitcast(E4M3FN), in1=scale[:, 0, :], op=ALU.mult
             )
 
-        def widen_block(g, j):
-            if j == 0:
-                new_natural(g)
-            c = slice(j * D, (j + 1) * D)
-            nc.vector.tensor_tensor(out=natural[g][:, c], in0=x8[g][:, c].bitcast(F8), in1=scale[:, 0, :], op=ALU.mult)
+        def widen(g):
+            new_plain(g)
+            nc.vector.tensor_tensor(
+                out=plain[g][:], in0=x8[g][:].bitcast(E4M3FN), in1=scale[:].rearrange("p j k -> p (j k)"), op=ALU.mult
+            )
 
-        def turn(key, h):
-            b = bank(("xt", key, h), [P, 2, 2, P])
-            words = natural[key][:].bitcast(F32)
+        def turn(key, half):
+            b = bank((key, half), [P, 2, 2, P])
+            words = plain[key][:].bitcast(F32)
             for jj in range(2):
-                base = 256 * (2 * h + jj)
+                first = (2 * half + jj) * (K // 2)
                 for u in range(2):
-                    nc.tensor.transpose(b[:, jj, u, :], words[:, base + u : base + 256 : 2], ident[:])
+                    nc.tensor.transpose(b[:, jj, u, :], words[:, first + u : first + K // 2 : 2], ident[:])
 
-        def turn_out(key, h, vec=False):
-            if h == 0:
-                inter[key] = work.tile([P, 4 * D], BF16, name="inter", tag="inter", align_bytes=64)
-            dst = inter[key][:, 1024 * h : 1024 * (h + 1)].bitcast(F32).rearrange("p (j r u) -> p j r u", j=2, u=2)
-            src = banks["xt", key, h][:].rearrange("p j u r -> p j r u")
-            if vec:
-                nc.vector.tensor_copy(out=dst, in_=src)
-            else:
-                nc.scalar.copy(out=dst, in_=src)
+        def turn_out(key, half):
+            if half == 0:
+                packed[key] = work.tile([P, SETS * P * PACK], BF16, name="packed", tag="packed", align_bytes=64)
+            cols = slice(2 * P * PACK * half, 2 * P * PACK * (half + 1))
+            nc.scalar.copy(
+                out=packed[key][:, cols].bitcast(F32).rearrange("p (j r u) -> p j r u", j=2, u=2),
+                in_=banks[key, half][:].rearrange("p j u r -> p j r u"),
+            )
 
         def quantize(key, src, pool, tag):
-            codes[key] = pool.tile([P, D], U32, name="c_" + tag, tag="c_" + tag, align_bytes=64)
-            scales[key] = pool.tile([P, D], U8, name="s_" + tag, tag="s_" + tag, align_bytes=64)
-            nc.vector.quantize_mx(out=codes[key][:].bitcast(FP8X4), scales=scales[key][:], in_=src[:])
+            codes[key] = pool.tile([P, SETS * P], U32, name="codes_" + tag, tag="codes_" + tag, align_bytes=64)
+            scale_bytes[key] = pool.tile([P, SETS * P], U8, name="bytes_" + tag, tag="bytes_" + tag, align_bytes=64)
+            nc.vector.quantize_mx(out=codes[key][:].bitcast(E4M3FN_X4), scales=scale_bytes[key][:], in_=src[:])
 
-        def mm(dst, lkey, lcols, rkey, rcols):
+        def multiply(dst, left, left_cols, right, right_cols):
             nc.tensor.matmul_mx(
                 out=dst,
-                lhsT=codes[lkey][:, lcols].bitcast(FP8X4),
-                lhsT_scale=scales[lkey][:, lcols],
-                rhs=codes[rkey][:, rcols].bitcast(FP8X4),
-                rhs_scale=scales[rkey][:, rcols],
+                lhsT=codes[left][:, left_cols].bitcast(E4M3FN_X4),
+                lhsT_scale=scale_bytes[left][:, left_cols],
+                rhs=codes[right][:, right_cols].bitcast(E4M3FN_X4),
+                rhs_scale=scale_bytes[right][:, right_cols],
                 start=True,
                 stop=True,
             )
 
-        planes, h_sb, y_sb, o_ch, o_tok = {}, {}, {}, {}, {}
+        h_planes, h_packed = {}, {}
 
         def layer1(g, t):
-            b = bank(("h", g, t), [P, GROUP])
-            mm(b[:], "W0", slice(P * t, P * (t + 1)), g, slice(0, GROUP))
+            b = bank(("hidden", g, t), [P, GROUP])
+            multiply(b[:], "W0", slice(P * t, P * (t + 1)), g, slice(0, GROUP))
 
-        def hidden(g, t, vec=False):
+        def hidden(g, t):
             if t == 0:
-                planes[g] = work.tile([P, 4, GROUP], BF16, name="planes", tag="planes", align_bytes=64)
-            b = banks["h", g, t]
-            if vec:
-                nc.vector.tensor_scalar(
-                    out=planes[g][:, t, :], in0=b[:], scalar1=b0f[:, t : t + 1], scalar2=0.0, op0=ALU.add, op1=ALU.max
-                )
-            else:
-                nc.scalar.activation(out=planes[g][:, t, :], in_=b[:], func=ACT.Relu, bias=b0f[:, t : t + 1])
+                h_planes[g] = work.tile([P, PACK, GROUP], BF16, name="h_planes", tag="h_planes", align_bytes=64)
+            nc.scalar.activation(
+                out=h_planes[g][:, t, :], in_=banks["hidden", g, t][:], func=ACT.Relu, bias=b0_cols[:, t : t + 1]
+            )
 
         def interleave(g):
-            h_sb[g] = work.tile([P, 4 * D], BF16, name="h_sb", tag="h_sb", align_bytes=64)
-            dst = h_sb[g][:].rearrange("p (c i t) -> p c t i", i=4, t=4)
-            nc.vector.tensor_copy(out=dst, in_=planes[g][:].rearrange("p t (c i) -> p c t i", i=4))
+            h_packed[g] = work.tile([P, GROUP * PACK], BF16, name="h_packed", tag="h_packed", align_bytes=64)
+            nc.vector.tensor_copy(
+                out=h_packed[g][:].rearrange("p (c i t) -> p c t i", i=4, t=PACK),
+                in_=h_planes[g][:].rearrange("p t (c i) -> p c t i", i=4),
+            )
 
-        def layer2_ch(g, e):
-            b = bank(("y", g, e), [P, GROUP])
-            mm(b[:], "W1", slice(P * e, P * (e + 1)), ("h", g), slice(0, GROUP))
+        y, out_by_channels, out_by_tokens = {}, {}, {}
 
-        def bias_ch(g, e, vec=False):
+        def layer2_by_channels(g, e):
+            b = bank(("channels", g, e), [P, GROUP])
+            multiply(b[:], "W1", slice(P * e, P * (e + 1)), ("h", g), slice(0, GROUP))
+
+        def bias_by_channels(g, e, on_vector=False):
             if e == 0:
-                y_sb[g] = work.tile([P, 2, GROUP], F32, name="y_sb", tag="y_sb", align_bytes=64)
-            b = banks["y", g, e]
-            if vec:
+                y[g] = work.tile([P, 2, GROUP], F32, name="y", tag="y", align_bytes=64)
+            src = banks["channels", g, e]
+            bias = b1_cols[:, 0, e : e + 1]
+            if on_vector:
                 nc.vector.tensor_scalar(
-                    out=y_sb[g][:, e, :], in0=b[:], scalar1=b1f[:, e : e + 1], scalar2=0.0, op0=ALU.add, op1=ALU.max
+                    out=y[g][:, e, :], in0=src[:], scalar1=bias, scalar2=0.0, op0=ALU.add, op1=ALU.max
                 )
             else:
-                nc.scalar.activation(out=y_sb[g][:, e, :], in_=b[:], func=ACT.Relu, bias=b1f[:, e : e + 1])
+                nc.scalar.activation(out=y[g][:, e, :], in_=src[:], func=ACT.Relu, bias=bias)
 
-        def back(g, h):
-            b = bank(("t", g, h), [P, 2, 2, P])
+        def back(g, half):
+            b = bank(("back", g, half), [P, 2, 2, P])
             for jj in range(2):
-                j = 2 * h + jj
+                j = 2 * half + jj
                 for e in range(2):
-                    nc.tensor.transpose(b[:, jj, e, :], y_sb[g][:, e, P * j : P * (j + 1)], ident[:])
+                    nc.tensor.transpose(b[:, jj, e, :], y[g][:, e, P * j : P * (j + 1)], ident[:])
 
-
-        def back_out(g, h, vec=False):
-            if h == 0:
-                o_ch[g] = work.tile([P, 4, HALF], F32, name="o_ch", tag="o_ch", align_bytes=64)
-            dst = o_ch[g][:, 2 * h : 2 * h + 2, :].rearrange("p j (m e) -> p j m e", e=2)
-            src = banks["t", g, h][:].rearrange("p j e m -> p j m e")
-            if vec:
+        def back_out(g, half, on_vector=False):
+            if half == 0:
+                out_by_channels[g] = work.tile([P, SETS, HALF], F32, name="out_ch", tag="out_ch", align_bytes=64)
+            dst = out_by_channels[g][:, 2 * half : 2 * half + 2, :].rearrange("p j (m e) -> p j m e", e=2)
+            src = banks["back", g, half][:].rearrange("p j e m -> p j m e")
+            if on_vector:
                 nc.vector.tensor_copy(out=dst, in_=src)
             else:
                 nc.scalar.copy(out=dst, in_=src)
 
-        def layer2_tok(g, h):
-            b = bank(("o", g, h), [P, 2, HALF])
+        def layer2_by_tokens(g, half):
+            b = bank(("tokens", g, half), [P, 2, HALF])
             for jj in range(2):
-                j = 2 * h + jj
-                mm(b[:, jj, :], ("h", g), slice(P * j, P * (j + 1)), "W1", slice(HALF, D))
+                j = 2 * half + jj
+                multiply(b[:, jj, :], ("h", g), slice(P * j, P * (j + 1)), "W1", slice(HALF, K))
 
-        def bias_tok(g, h):
-            if h == 0:
-                o_tok[g] = work.tile([P, 4, HALF], F32, name="o_tok", tag="o_tok", align_bytes=64)
-            nc.vector.tensor_tensor(
-                out=o_tok[g][:, 2 * h : 2 * h + 2, :], in0=banks["o", g, h][:], in1=b1t[:], op=ALU.add
-            )
+        def bias_by_tokens(g, half):
+            if half == 0:
+                out_by_tokens[g] = work.tile([P, SETS, HALF], F32, name="out_tok", tag="out_tok", align_bytes=64)
+            dst = out_by_tokens[g][:, 2 * half : 2 * half + 2, :]
+            nc.vector.tensor_tensor(out=dst, in0=banks["tokens", g, half][:], in1=b1_spread[:], op=ALU.add)
 
-        def relu_tok(g, eng, j0=0, j1=4):
-            v = o_tok[g][:, j0:j1, :]
-            if eng == "V":
+        def relu_by_tokens(g, j0, j1, on_vector):
+            v = out_by_tokens[g][:, j0:j1, :]
+            if on_vector:
                 nc.vector.tensor_scalar_max(v, v, 0.0)
-            elif eng == "G":
-                nc.gpsimd.tensor_scalar(out=v, in0=v, scalar1=0.0, scalar2=0.0, op0=ALU.max, op1=ALU.add)
             else:
                 nc.scalar.activation(out=v, in_=v, func=ACT.Relu)
 
-        def store(g, tok, j0=0, j1=4):
-            rows = out[g * GROUP : (g + 1) * GROUP, :].rearrange("(r j) c -> r j c", j=4)
-            if tok:
-                nc.sync.dma_start(out=rows[:, j0:j1, HALF:D], in_=o_tok[g][:, j0:j1, :])
-            else:
-                nc.sync.dma_start(out=rows[:, j0:j1, 0:HALF], in_=o_ch[g][:, j0:j1, :])
+        def store(g, tile, channels, j0=0, j1=SETS):
+            dst = out[g * GROUP : (g + 1) * GROUP, channels].rearrange("(r j) c -> r j c", j=SETS)
+            nc.sync.dma_start(out=dst[:, j0:j1, :], in_=tile[g][:, j0:j1, :])
 
-        def ok(g):
-            return 0 <= g < NG
+        first_half, second_half = slice(0, HALF), slice(HALF, K)
 
-        on_vector = [(NG - 1, 3)]
+        for half in range(2):
+            mask_half("W0", w0_rows, m0_rows, half)
         spread_scale()
-        for j in range(4):
-            widen_block(0, j)
-            if j % 2 == 1:
-                turn(0, j // 2)
-                turn_out(0, j // 2)
-        for h in range(2):
-            mask_w("W0", "w0", "m0", h)
-            turn("W0", h)
-            turn_out("W0", h)
-        widen_block(1, 0)
-        widen_block(1, 1)
-        quantize(0, inter[0], work, "x")
-        quantize("W0", inter["W0"], keep, "w0")
-        widen_block(1, 2)
-        widen_block(1, 3)
+        for half in range(2):
+            turn("W0", half)
+            turn_out("W0", half)
+        for half in range(2):
+            widen_set(0, 2 * half)
+            widen_set(0, 2 * half + 1)
+            turn(0, half)
+            turn_out(0, half)
+        quantize("W0", packed["W0"], keep, "W0")
+        nc.scalar.copy(out=b0_cols[:], in_=b0_bf16[:])
+        nc.scalar.copy(out=b1_cols[:], in_=b1_bf16[:])
+        widen_set(1, 0)
+        widen_set(1, 1)
+        quantize(0, packed[0], work, "x")
+        widen_set(1, 2)
+        widen_set(1, 3)
         for t in range(3):
             layer1(0, t)
-        turn(1, 0)
-        turn(1, 1)
-        for h in range(2):
-            mask_w("W1", "w1", "m1", h)
+        for half in range(2):
+            turn(1, half)
+        for half in range(2):
+            mask_half("W1", w1_rows, m1_rows, half)
 
-        for i in range(NG):
-            cur, nxt, nx2, prv, pp = ok(i), ok(i + 1), ok(i + 2), ok(i - 1), ok(i - 2)
-            if prv:
-                layer2_tok(i - 1, 0)
+        for i in range(N_GROUPS):
+            has_next, has_prev = i + 1 < N_GROUPS, i >= 1
+            widens, gives_back = i + 2 < N_GROUPS, i >= 2
+            if has_prev:
+                layer2_by_tokens(i - 1, 0)
             layer1(i, 3)
-            if prv:
-                layer2_tok(i - 1, 1)
-            if nx2:
+            if has_prev:
+                layer2_by_tokens(i - 1, 1)
+            if widens:
                 widen(i + 2)
-            hidden(i, 0, (i, 0) in on_vector)
-            hidden(i, 1, (i, 1) in on_vector)
-            if nxt:
+            hidden(i, 0)
+            hidden(i, 1)
+            if has_next:
                 turn_out(i + 1, 0)
                 turn_out(i + 1, 1)
             if i == 0:
                 spread_b1()
-            hidden(i, 2, (i, 2) in on_vector)
-            hidden(i, 3, (i, 3) in on_vector)
-            if prv:
-                bias_tok(i - 1, 0)
-            if nxt:
-                quantize(i + 1, inter[i + 1], work, "x")
-            if prv:
-                bias_tok(i - 1, 1)
+            hidden(i, 2)
+            hidden(i, 3)
+            if has_prev:
+                bias_by_tokens(i - 1, 0)
+            if has_next:
+                quantize(i + 1, packed[i + 1], work, "x")
+            if has_prev:
+                bias_by_tokens(i - 1, 1)
             if i == 0:
-                for h in range(2):
-                    turn("W1", h)
-                    turn_out("W1", h)
+                for half in range(2):
+                    turn("W1", half)
+                    turn_out("W1", half)
             interleave(i)
             if i == 0:
-                quantize("W1", inter["W1"], keep, "w1")
-            split = 4 if i == NG - 2 else 2 if i == NG - 1 else 2
-            if prv:
-                relu_tok(i - 1, "V", 0, split)
-            quantize(("h", i), h_sb[i], work, "h")
-            if pp:
+                quantize("W1", packed["W1"], keep, "W1")
+            if has_prev:
+                on_vector = sets_with_relu_on_vector(i - 1)
+                relu_by_tokens(i - 1, 0, on_vector, True)
+            quantize(("h", i), h_packed[i], work, "h")
+            if gives_back:
                 back(i - 2, 0)
                 back(i - 2, 1)
-            if prv:
-                layer2_ch(i - 1, 0)
-                layer2_ch(i - 1, 1)
-            if pp:
+            if has_prev:
+                layer2_by_channels(i - 1, 0)
+                layer2_by_channels(i - 1, 1)
+            if gives_back:
                 back_out(i - 2, 0)
                 back_out(i - 2, 1)
-                store(i - 2, False)
-            if prv:
-                bias_ch(i - 1, 0)
-                bias_ch(i - 1, 1)
-                if split < 4:
-                    relu_tok(i - 1, "S", split, 4)
-                store(i - 1, True)
-            if nx2:
+                store(i - 2, out_by_channels, first_half)
+            if has_prev:
+                bias_by_channels(i - 1, 0)
+                bias_by_channels(i - 1, 1)
+                if on_vector < SETS:
+                    relu_by_tokens(i - 1, on_vector, SETS, False)
+                store(i - 1, out_by_tokens, second_half)
+            if widens:
                 turn(i + 2, 0)
                 turn(i + 2, 1)
-            if nxt:
+            if has_next:
                 for t in range(3):
                     layer1(i + 1, t)
-        g = NG - 1
+
+        g = N_GROUPS - 1
         back(g - 1, 0)
         back(g - 1, 1)
-        layer2_tok(g, 0)
-        layer2_ch(g, 0)
-        layer2_ch(g, 1)
-        layer2_tok(g, 1)
+        layer2_by_tokens(g, 0)
+        layer2_by_channels(g, 0)
+        layer2_by_channels(g, 1)
+        layer2_by_tokens(g, 1)
         back_out(g - 1, 0)
-        back_out(g - 1, 1, False)
-        store(g - 1, False)
-        bias_tok(g, 0)
-        bias_ch(g, 0)
-        bias_ch(g, 1, True)
+        back_out(g - 1, 1)
+        store(g - 1, out_by_channels, first_half)
+        bias_by_tokens(g, 0)
+        bias_by_channels(g, 0)
+        bias_by_channels(g, 1, on_vector=True)
         back(g, 0)
-        relu_tok(g, "S", 0, 2)
-        store(g, True, 0, 2)
-        bias_tok(g, 1)
+        relu_by_tokens(g, 0, 2, False)
+        store(g, out_by_tokens, second_half, 0, 2)
+        bias_by_tokens(g, 1)
         back(g, 1)
         back_out(g, 0)
-        store(g, False, 0, 2)
-        relu_tok(g, "V", 2, 4)
-        store(g, True, 2, 4)
-        back_out(g, 1, True)
-        store(g, False, 2, 4)
+        store(g, out_by_channels, first_half, 0, 2)
+        relu_by_tokens(g, 2, SETS, True)
+        store(g, out_by_tokens, second_half, 2, SETS)
+        back_out(g, 1, on_vector=True)
+        store(g, out_by_channels, first_half, 2, SETS)

from contextlib import ExitStack

import concourse.mybir as mybir
from concourse.masks import make_identity

F32 = mybir.dt.float32
BF16 = mybir.dt.bfloat16
U32 = mybir.dt.uint32
U8 = mybir.dt.uint8
E4M3FN = mybir.dt.float8_e4m3fn
E4M3FN_X4 = mybir.dt.float8_e4m3fn_x4
ALU = mybir.AluOpType
ACT = mybir.ActivationFunctionType

P = 128
PACK = 4
SETS = 4
K = 512
HALF = K // 2
N_TOKENS = 8192
GROUP = SETS * P
N_GROUPS = N_TOKENS // GROUP

FLOPS = 2 * (2 * N_TOKENS * K * K)


def sets_with_relu_on_vector(g):
    if g == N_GROUPS - 3:
        return 4
    return 3 if g % 4 == 3 and g < N_GROUPS - 3 else 2


def tile_patchedsparsenetwork_pa_t_kernel(tc, x_bytes, x_scale, W0, b0, m0, W1, b1, m1, out):
    nc = tc.nc
    with ExitStack() as ctx:
        keep = ctx.enter_context(tc.tile_pool(name="keep", bufs=1))
        work = ctx.enter_context(tc.tile_pool(name="work", bufs=3))
        psum = ctx.enter_context(tc.psum_pool(name="psum", bufs=8))
        ctx.enter_context(tc.manual_schedule())

        scale_cols = keep.tile([P, PACK], F32, name="scale_cols", align_bytes=64)
        nc.scalar.dma_start(out=scale_cols[:], in_=x_scale.rearrange("o (n m) -> (o n) m", m=PACK))
        warm = keep.tile([P, 1], F32, name="warm", align_bytes=64)
        nc.vector.memset(warm[:], 0.0)
        nc.scalar.activation(out=warm[:], in_=warm[:], func=ACT.Relu)
        b0_bf16 = keep.tile([P, PACK], BF16, name="b0_bf16", align_bytes=64)
        nc.scalar.dma_start(out=b0_bf16[:], in_=b0.rearrange("(p t) -> p t", t=PACK))
        b1_bf16 = keep.tile([P, 2, 2], BF16, name="b1_bf16", align_bytes=64)
        nc.scalar.dma_start(out=b1_bf16[:], in_=b1.rearrange("(h m e) -> m h e", h=2, e=2))

        w0_rows = keep.tile([P, SETS, K], BF16, name="w0_rows", align_bytes=64)
        m0_rows = keep.tile([P, SETS, K], BF16, name="m0_rows", align_bytes=64)
        w1_rows = keep.tile([P, SETS, K], BF16, name="w1_rows", align_bytes=64)
        m1_rows = keep.tile([P, SETS, K], BF16, name="m1_rows", align_bytes=64)

        def load_half(dst, src, half):
            nc.sync.dma_start(out=dst[:, 2 * half : 2 * half + 2, :], in_=src)

        def layer1_rows(w, half):
            return w.rearrange("(m s) k -> m s k", s=SETS)[:, 2 * half : 2 * half + 2, :]

        def layer2_rows(w, half):
            part = w[half * HALF : (half + 1) * HALF, :]
            return part.rearrange("(m s) k -> m s k", s=2) if half == 0 else part.rearrange("(s m) k -> m s k", s=2)

        x8 = {}

        def load_x(g):
            x8[g] = keep.tile([P, SETS * K], U8, name="x8_%d" % g, align_bytes=64)
            tokens = x_bytes[g * GROUP : (g + 1) * GROUP, :]
            nc.sync.dma_start(out=x8[g][:], in_=tokens.rearrange("(r j) k -> r (j k)", j=SETS))

        for half in range(2):
            load_half(w0_rows, layer1_rows(W0, half), half)
            load_half(m0_rows, layer1_rows(m0, half), half)
        load_x(0)
        load_x(1)
        for half in range(2):
            load_half(w1_rows, layer2_rows(W1, half), half)
            load_half(m1_rows, layer2_rows(m1, half), half)
        for g in range(2, N_GROUPS):
            load_x(g)

        ident = keep.tile([P, P], F32, name="ident", align_bytes=64)
        make_identity(nc, ident[:])

        b0_cols = keep.tile([P, PACK], F32, name="b0_cols", align_bytes=64)
        b1_cols = keep.tile([P, 2, 2], F32, name="b1_cols", align_bytes=64)
        scale = keep.tile([P, SETS, K], F32, name="scale", align_bytes=64)
        b1_spread = keep.tile([P, 2, HALF], F32, name="b1_spread", align_bytes=64)

        banks = {}

        def bank(key, shape):
            banks[key] = psum.tile(shape, F32, name="bank", tag="bank")
            return banks[key]

        def spread_scale():
            b = bank("scale", [P, PACK, P])
            for m in range(PACK):
                nc.tensor.transpose(b[:, m, :], scale_cols[:, m : m + 1].to_broadcast([P, P]), ident[:])
            nc.scalar.copy(
                out=scale[:, 0, :].rearrange("p (n m) -> p n m", m=PACK), in_=b[:].rearrange("p m n -> p n m")
            )
            nc.scalar.copy(out=scale[:, 1:SETS, :], in_=scale[:, 0:1, :].to_broadcast([P, SETS - 1, K]))

        def spread_b1():
            b = bank("b1", [P, 2, P])
            for e in range(2):
                nc.tensor.transpose(b[:, e, :], b1_cols[:, 1, e : e + 1].to_broadcast([P, P]), ident[:])
            for copy in range(2):
                nc.scalar.copy(
                    out=b1_spread[:, copy, :].rearrange("p (n e) -> p n e", e=2), in_=b[:].rearrange("p e n -> p n e")
                )

        plain, packed, codes, scale_bytes = {}, {}, {}, {}

        def new_plain(key):
            plain[key] = work.tile([P, SETS * K], BF16, name="plain", tag="plain", align_bytes=64)

        def mask_half(key, w, m, half):
            if half == 0:
                new_plain(key)
            sets = slice(2 * half, 2 * half + 2)
            dst = plain[key][:].rearrange("p (s k) -> p s k", s=SETS)[:, sets, :]
            nc.vector.tensor_tensor(out=dst, in0=w[:, sets, :], in1=m[:, sets, :], op=ALU.mult)

        def widen_set(g, j):
            if j == 0:
                new_plain(g)
            cols = slice(j * K, (j + 1) * K)
            nc.vector.tensor_tensor(
                out=plain[g][:, cols], in0=x8[g][:, cols].bitcast(E4M3FN), in1=scale[:, 0, :], op=ALU.mult
            )

        def widen(g):
            new_plain(g)
            nc.vector.tensor_tensor(
                out=plain[g][:], in0=x8[g][:].bitcast(E4M3FN), in1=scale[:].rearrange("p j k -> p (j k)"), op=ALU.mult
            )

        def turn(key, half):
            b = bank((key, half), [P, 2, 2, P])
            words = plain[key][:].bitcast(F32)
            for jj in range(2):
                first = (2 * half + jj) * (K // 2)
                for u in range(2):
                    nc.tensor.transpose(b[:, jj, u, :], words[:, first + u : first + K // 2 : 2], ident[:])

        def turn_out(key, half):
            if half == 0:
                packed[key] = work.tile([P, SETS * P * PACK], BF16, name="packed", tag="packed", align_bytes=64)
            cols = slice(2 * P * PACK * half, 2 * P * PACK * (half + 1))
            nc.scalar.copy(
                out=packed[key][:, cols].bitcast(F32).rearrange("p (j r u) -> p j r u", j=2, u=2),
                in_=banks[key, half][:].rearrange("p j u r -> p j r u"),
            )

        def quantize(key, src, pool, tag):
            codes[key] = pool.tile([P, SETS * P], U32, name="codes_" + tag, tag="codes_" + tag, align_bytes=64)
            scale_bytes[key] = pool.tile([P, SETS * P], U8, name="bytes_" + tag, tag="bytes_" + tag, align_bytes=64)
            nc.vector.quantize_mx(out=codes[key][:].bitcast(E4M3FN_X4), scales=scale_bytes[key][:], in_=src[:])

        def multiply(dst, left, left_cols, right, right_cols):
            nc.tensor.matmul_mx(
                out=dst,
                lhsT=codes[left][:, left_cols].bitcast(E4M3FN_X4),
                lhsT_scale=scale_bytes[left][:, left_cols],
                rhs=codes[right][:, right_cols].bitcast(E4M3FN_X4),
                rhs_scale=scale_bytes[right][:, right_cols],
                start=True,
                stop=True,
            )

        h_planes, h_packed = {}, {}

        def layer1(g, t):
            b = bank(("hidden", g, t), [P, GROUP])
            multiply(b[:], "W0", slice(P * t, P * (t + 1)), g, slice(0, GROUP))

        def hidden(g, t):
            if t == 0:
                h_planes[g] = work.tile([P, PACK, GROUP], BF16, name="h_planes", tag="h_planes", align_bytes=64)
            nc.scalar.activation(
                out=h_planes[g][:, t, :], in_=banks["hidden", g, t][:], func=ACT.Relu, bias=b0_cols[:, t : t + 1]
            )

        def interleave(g):
            h_packed[g] = work.tile([P, GROUP * PACK], BF16, name="h_packed", tag="h_packed", align_bytes=64)
            nc.vector.tensor_copy(
                out=h_packed[g][:].rearrange("p (c i t) -> p c t i", i=4, t=PACK),
                in_=h_planes[g][:].rearrange("p t (c i) -> p c t i", i=4),
            )

        y, out_by_channels, out_by_tokens = {}, {}, {}

        def layer2_by_channels(g, e):
            b = bank(("channels", g, e), [P, GROUP])
            multiply(b[:], "W1", slice(P * e, P * (e + 1)), ("h", g), slice(0, GROUP))

        def bias_by_channels(g, e, on_vector=False):
            if e == 0:
                y[g] = work.tile([P, 2, GROUP], F32, name="y", tag="y", align_bytes=64)
            src = banks["channels", g, e]
            bias = b1_cols[:, 0, e : e + 1]
            if on_vector:
                nc.vector.tensor_scalar(
                    out=y[g][:, e, :], in0=src[:], scalar1=bias, scalar2=0.0, op0=ALU.add, op1=ALU.max
                )
            else:
                nc.scalar.activation(out=y[g][:, e, :], in_=src[:], func=ACT.Relu, bias=bias)

        def back(g, half):
            b = bank(("back", g, half), [P, 2, 2, P])
            for jj in range(2):
                j = 2 * half + jj
                for e in range(2):
                    nc.tensor.transpose(b[:, jj, e, :], y[g][:, e, P * j : P * (j + 1)], ident[:])

        def back_out(g, half, on_vector=False):
            if half == 0:
                out_by_channels[g] = work.tile([P, SETS, HALF], F32, name="out_ch", tag="out_ch", align_bytes=64)
            dst = out_by_channels[g][:, 2 * half : 2 * half + 2, :].rearrange("p j (m e) -> p j m e", e=2)
            src = banks["back", g, half][:].rearrange("p j e m -> p j m e")
            if on_vector:
                nc.vector.tensor_copy(out=dst, in_=src)
            else:
                nc.scalar.copy(out=dst, in_=src)

        def layer2_by_tokens(g, half):
            b = bank(("tokens", g, half), [P, 2, HALF])
            for jj in range(2):
                j = 2 * half + jj
                multiply(b[:, jj, :], ("h", g), slice(P * j, P * (j + 1)), "W1", slice(HALF, K))

        def bias_by_tokens(g, half):
            if half == 0:
                out_by_tokens[g] = work.tile([P, SETS, HALF], F32, name="out_tok", tag="out_tok", align_bytes=64)
            dst = out_by_tokens[g][:, 2 * half : 2 * half + 2, :]
            nc.vector.tensor_tensor(out=dst, in0=banks["tokens", g, half][:], in1=b1_spread[:], op=ALU.add)

        def relu_by_tokens(g, j0, j1, on_vector):
            v = out_by_tokens[g][:, j0:j1, :]
            if on_vector:
                nc.vector.tensor_scalar_max(v, v, 0.0)
            else:
                nc.scalar.activation(out=v, in_=v, func=ACT.Relu)

        def store(g, tile, channels, j0=0, j1=SETS):
            dst = out[g * GROUP : (g + 1) * GROUP, channels].rearrange("(r j) c -> r j c", j=SETS)
            nc.sync.dma_start(out=dst[:, j0:j1, :], in_=tile[g][:, j0:j1, :])

        first_half, second_half = slice(0, HALF), slice(HALF, K)

        for half in range(2):
            mask_half("W0", w0_rows, m0_rows, half)
        spread_scale()
        for half in range(2):
            turn("W0", half)
            turn_out("W0", half)
        for half in range(2):
            widen_set(0, 2 * half)
            widen_set(0, 2 * half + 1)
            turn(0, half)
            turn_out(0, half)
        quantize("W0", packed["W0"], keep, "W0")
        nc.scalar.copy(out=b0_cols[:], in_=b0_bf16[:])
        nc.scalar.copy(out=b1_cols[:], in_=b1_bf16[:])
        widen_set(1, 0)
        widen_set(1, 1)
        quantize(0, packed[0], work, "x")
        widen_set(1, 2)
        widen_set(1, 3)
        for t in range(3):
            layer1(0, t)
        for half in range(2):
            turn(1, half)
        for half in range(2):
            mask_half("W1", w1_rows, m1_rows, half)

        for i in range(N_GROUPS):
            has_next, has_prev = i + 1 < N_GROUPS, i >= 1
            widens, gives_back = i + 2 < N_GROUPS, i >= 2
            if has_prev:
                layer2_by_tokens(i - 1, 0)
            layer1(i, 3)
            if has_prev:
                layer2_by_tokens(i - 1, 1)
            if widens:
                widen(i + 2)
            hidden(i, 0)
            hidden(i, 1)
            if has_next:
                turn_out(i + 1, 0)
                turn_out(i + 1, 1)
            if i == 0:
                spread_b1()
            hidden(i, 2)
            hidden(i, 3)
            if has_prev:
                bias_by_tokens(i - 1, 0)
            if has_next:
                quantize(i + 1, packed[i + 1], work, "x")
            if has_prev:
                bias_by_tokens(i - 1, 1)
            if i == 0:
                for half in range(2):
                    turn("W1", half)
                    turn_out("W1", half)
            interleave(i)
            if i == 0:
                quantize("W1", packed["W1"], keep, "W1")
            if has_prev:
                on_vector = sets_with_relu_on_vector(i - 1)
                relu_by_tokens(i - 1, 0, on_vector, True)
            quantize(("h", i), h_packed[i], work, "h")
            if gives_back:
                back(i - 2, 0)
                back(i - 2, 1)
            if has_prev:
                layer2_by_channels(i - 1, 0)
                layer2_by_channels(i - 1, 1)
            if gives_back:
                back_out(i - 2, 0)
                back_out(i - 2, 1)
                store(i - 2, out_by_channels, first_half)
            if has_prev:
                bias_by_channels(i - 1, 0)
                bias_by_channels(i - 1, 1)
                if on_vector < SETS:
                    relu_by_tokens(i - 1, on_vector, SETS, False)
                store(i - 1, out_by_tokens, second_half)
            if widens:
                turn(i + 2, 0)
                turn(i + 2, 1)
            if has_next:
                for t in range(3):
                    layer1(i + 1, t)

        g = N_GROUPS - 1
        back(g - 1, 0)
        back(g - 1, 1)
        layer2_by_tokens(g, 0)
        layer2_by_channels(g, 0)
        layer2_by_channels(g, 1)
        layer2_by_tokens(g, 1)
        back_out(g - 1, 0)
        back_out(g - 1, 1)
        store(g - 1, out_by_channels, first_half)
        bias_by_tokens(g, 0)
        bias_by_channels(g, 0)
        bias_by_channels(g, 1, on_vector=True)
        back(g, 0)
        relu_by_tokens(g, 0, 2, False)
        store(g, out_by_tokens, second_half, 0, 2)
        bias_by_tokens(g, 1)
        back(g, 1)
        back_out(g, 0)
        store(g, out_by_channels, first_half, 0, 2)
        relu_by_tokens(g, 2, SETS, True)
        store(g, out_by_tokens, second_half, 2, SETS)
        back_out(g, 1, on_vector=True)
        store(g, out_by_channels, first_half, 2, SETS)
